import numpy as np
import ml_dtypes


def mxq(x, axis, fmt="e4m3"):
    dtype, down = {"e4m3": (ml_dtypes.float8_e4m3fn, 7), "e5m2": (ml_dtypes.float8_e5m2, 14)}[fmt]
    v = np.moveaxis(np.asarray(x, np.float32).astype(ml_dtypes.bfloat16).astype(np.float64), axis, -1)
    blocks = v.reshape(v.shape[:-1] + (-1, 32))
    amax = np.abs(blocks).max(-1, keepdims=True)
    byte = np.maximum(np.where(amax > 0, np.frexp(amax)[1] - 1 + 127, 0) - down, 1)
    scale = np.exp2(byte - 127.0)
    codes = (blocks / scale).astype(np.float32).astype(dtype).astype(np.float64)
    return np.moveaxis((codes * scale).reshape(v.shape), -1, axis)


WIDE = False


def mx_kscale(k):
    if not WIDE:
        return np.ones(k)
    levels = np.array([20, -20, 10, -10, 0])
    a = np.random.permutation(np.resize(levels, k // 512 * 4)).reshape(k // 512, 4)
    idx = np.arange(k)
    return np.exp2(a[idx // 512, idx % 128 // 32])


BF16 = ml_dtypes.bfloat16


def bf(x):
    return np.asarray(x, np.float32).astype(BF16)


def f64(x):
    return np.asarray(x).astype(np.float64)


B, C, H, W, K, R = 4, 1024, 32, 32, 1024, 8
EPS = 1e-8
GS = 128.0


def setup_inputs():
    u = mx_kscale(K)[:, None]
    core = np.random.standard_normal((R, C)) / np.sqrt(R)
    fa = np.random.standard_normal((B, R, H, W))
    pa = np.random.standard_normal((K, R))
    features = 0.5 * np.random.standard_normal((B, C, H, W))
    prototypes = 0.5 * np.random.standard_normal((K, C))
    for r in range(R):
        features += core[r][None, :, None, None] * fa[:, r][:, None]
        prototypes += pa[:, r][:, None] * core[r][None, :]
    g = np.random.standard_normal((B, K, H, W)) * np.exp2(np.random.randint(-12, 1, (B, 1, H, W))) * GS
    return {"features": bf(features), "prototypes": bf(prototypes * 0.5 / np.sqrt(C) / u), "grad_out": bf(g)}


def reference(features, prototypes, grad_out):
    f = f64(features).reshape(B, C, H * W)
    p = f64(prototypes)
    g = f64(grad_out).reshape(B, K, H * W)
    p_norm = np.sqrt(np.sum(p * p, axis=1))
    f_sq = np.sum(f * f, axis=1)
    gs = g / p_norm[None, :, None]
    m = mxq(p, 0, "e4m3").T @ mxq(gs, 1, "e5m2")
    a = np.sum(f * m, axis=1) / f_sq
    res = (m - f * a[:, None, :]) / np.sqrt(f_sq)[:, None, :]
    return res.reshape(B, C, H, W)

@@ -1,0 +1,300 @@
+from contextlib import ExitStack
+
+import concourse.mybir as mybir
+from concourse.masks import make_identity
+
+BF16 = mybir.dt.bfloat16
+F32 = mybir.dt.float32
+U32 = mybir.dt.uint32
+U8 = mybir.dt.uint8
+E4M3_X4 = mybir.dt.float8_e4m3fn_x4
+E5M2_X4 = mybir.dt.float8_e5m2_x4
+ALU = mybir.AluOpType
+ACT = mybir.ActivationFunctionType
+
+B, C, K, N = 4, 1024, 1024, 1024
+P = 128
+PACK = 4
+PASSES = K // (P * PACK)
+BANK = 512
+C_TILES = C // P
+BLOCKS = B * N // P
+BLOCKS_PER_BATCH = N // P
+CHUNK = 512
+BLOCKS_PER_CHUNK = CHUNK // P
+CHUNKS_PER_BATCH = N // CHUNK
+
+FLOPS = 2 * B * N * K * C
+
+
+def tile_globalprototype_t_kernel(tc, features, prototypes, grad_out, out):
+    nc = tc.nc
+
+    feat_dram = features.rearrange("b (i p) h w -> b p i (h w)", p=P)
+    out_dram = out.rearrange("b (i p) h w -> b p i (h w)", p=P)
+    grad_dram = grad_out.rearrange("b (s p j) h w -> b s p j (h w)", s=PASSES, p=P, j=PACK)
+    prot_dram = prototypes.rearrange("(s p j) c -> s p j c", s=PASSES, p=P, j=PACK)
+
+    with ExitStack() as stack:
+        const = stack.enter_context(tc.tile_pool(name="const", bufs=1))
+        loads = stack.enter_context(tc.tile_pool(name="loads", bufs=2))
+        quant = stack.enter_context(tc.tile_pool(name="quant", bufs=2))
+        work = stack.enter_context(tc.tile_pool(name="work", bufs=3))
+        unread = stack.enter_context(tc.tile_pool(name="unread", bufs=2))
+        stats = stack.enter_context(tc.tile_pool(name="stats", bufs=6))
+        stores = stack.enter_context(tc.tile_pool(name="stores", bufs=2))
+        psum_ft = stack.enter_context(tc.psum_pool(name="psum_ft", bufs=3))
+        psum_m = stack.enter_context(tc.psum_pool(name="psum_m", bufs=2))
+        psum_out = stack.enter_context(tc.psum_pool(name="psum_out", bufs=2))
+        stack.enter_context(tc.manual_schedule())
+
+        ident_bf16 = const.tile([P, P], BF16)
+        make_identity(nc, ident_bf16[:])
+        ident_f32 = const.tile([P, P], F32)
+        make_identity(nc, ident_f32[:])
+        minus_half = const.tile([P, PACK], F32)
+        nc.gpsimd.memset(minus_half[:], -0.5)
+
+        grad_of = {}
+        feat_of = {}
+
+        def load_grad(b):
+            grad_sb = loads.tile([P, PASSES, PACK, N], BF16)
+            for s in range(PASSES):
+                nc.sync.dma_start(out=grad_sb[:, s], in_=grad_dram[b, s])
+            grad_of[b] = grad_sb
+
+        def load_features(b):
+            feat_sb = loads.tile([P, C_TILES, N], BF16)
+            nc.sync.dma_start(out=feat_sb[:], in_=feat_dram[b])
+            feat_of[b] = feat_sb
+
+        prot_of = {}
+        for s in range(PASSES):
+            prot_sb = const.tile([P, PACK, C], BF16, name="prot_sb%d" % s)
+            nc.sync.dma_start(out=prot_sb[:], in_=prot_dram[s])
+            prot_of[s] = prot_sb
+        for b in range(2):
+            load_grad(b)
+            load_features(b)
+
+        def regroup(grouped, rows):
+            nc.vector.tensor_copy(
+                out=grouped.rearrange("p (c i) t -> p c t i", i=4),
+                in_=rows.rearrange("p t (c i) -> p c t i", i=4),
+            )
+
+        prot_codes = const.tile([P, PASSES * C], U32, align_bytes=64)
+        prot_scales = const.tile([P, PASSES * C], U8, align_bytes=64)
+        prot_grouped = {}
+        inv_pnorm = {}
+
+        def regroup_prototypes(s):
+            grouped = quant.tile([P, PACK * C], BF16, align_bytes=64)
+            regroup(grouped[:].rearrange("p (w t) -> p w t", t=PACK), prot_of[s][:])
+            prot_grouped[s] = grouped
+
+        def quantise_prototypes(s):
+            cols = slice(s * C, (s + 1) * C)
+            nc.vector.quantize_mx(
+                out=prot_codes[:, cols].bitcast(E4M3_X4),
+                scales=prot_scales[:, cols],
+                in_=prot_grouped[s][:],
+            )
+
+        def invert_norms(s, pnorm_sq):
+            inv = const.tile([P, PACK], F32, name="inv_pnorm%d" % s)
+            nc.gpsimd.tensor_tensor(out=inv[:], in0=pnorm_sq[:], in1=minus_half[:], op=ALU.pow)
+            inv_pnorm[s] = inv
+
+        pnorm_sq0 = const.tile([P, PACK], F32)
+        for j in range(PACK):
+            squares = unread.tile([P, C], BF16)
+            nc.scalar.activation(
+                out=squares[:], in_=prot_of[0][:, j, :], func=ACT.Square, accum_out=pnorm_sq0[:, j : j + 1]
+            )
+        invert_norms(0, pnorm_sq0)
+
+        regroup_prototypes(0)
+        pnorm_sq1 = const.tile([P, PACK], F32)
+        for j in range(PACK):
+            products = unread.tile([P, C], F32)
+            nc.vector.scalar_tensor_tensor(
+                out=products[:],
+                in0=prot_of[1][:, j, :],
+                scalar=1.0,
+                in1=prot_of[1][:, j, :],
+                op0=ALU.mult,
+                op1=ALU.mult,
+                accum_out=pnorm_sq1[:, j : j + 1],
+            )
+        invert_norms(1, pnorm_sq1)
+        quantise_prototypes(0)
+        regroup_prototypes(1)
+
+        scaled_of = {}
+        grouped_of = {}
+        codes_of = {}
+        scales_of = {}
+
+        def scale_grad(chunk, s):
+            b, part = divmod(chunk, CHUNKS_PER_BATCH)
+            if s == 0:
+                scaled = quant.tile([P, PASSES, PACK, CHUNK], BF16)
+                scaled_of[chunk] = scaled
+            for j in range(PACK):
+                nc.vector.tensor_scalar(
+                    out=scaled_of[chunk][:, s, j, :],
+                    in0=grad_of[b][:, s, j, part * CHUNK : (part + 1) * CHUNK],
+                    scalar1=inv_pnorm[s][:, j : j + 1],
+                    scalar2=None,
+                    op0=ALU.mult,
+                )
+
+        def regroup_grad(chunk, s):
+            if s == 0:
+                grouped = quant.tile([P, PASSES * CHUNK * PACK], BF16, align_bytes=64)
+                grouped_of[chunk] = grouped
+            by_pass = grouped_of[chunk][:].rearrange("p (s w t) -> p s w t", s=PASSES, t=PACK)
+            regroup(by_pass[:, s], scaled_of[chunk][:, s])
+
+        def quantise_grad(chunk):
+            codes = quant.tile([P, PASSES * CHUNK], U32, align_bytes=64)
+            scales = quant.tile([P, PASSES * CHUNK], U8, align_bytes=64)
+            nc.vector.quantize_mx(out=codes[:].bitcast(E5M2_X4), scales=scales[:], in_=grouped_of[chunk][:])
+            codes_of[chunk] = codes
+            scales_of[chunk] = scales
+
+        scale_grad(0, 0)
+        quantise_prototypes(1)
+        scale_grad(0, 1)
+        regroup_grad(0, 0)
+        regroup_grad(0, 1)
+
+        feat_t_of = {}
+        inv_fnorm_of = {}
+        inv_fsq_of = {}
+        ms_of = {}
+        neg_res_of = {}
+        out_sb_of = {}
+
+        def transpose_features(blk):
+            b, q = divmod(blk, BLOCKS_PER_BATCH)
+            feat_t = psum_ft.tile([P, C], BF16)
+            for i in range(C_TILES):
+                nc.tensor.transpose(
+                    out=feat_t[:, i * P : (i + 1) * P],
+                    in_=feat_of[b][:, i, q * P : (q + 1) * P],
+                    identity=ident_bf16[:],
+                )
+            squares = unread.tile([P, C], BF16)
+            fnorm_sq = stats.tile([P, 1], F32)
+            nc.scalar.activation(out=squares[:], in_=feat_t[:], func=ACT.Square, accum_out=fnorm_sq[:])
+            inv_fnorm = stats.tile([P, 1], F32)
+            nc.gpsimd.tensor_tensor(out=inv_fnorm[:], in0=fnorm_sq[:], in1=minus_half[:, 0:1], op=ALU.pow)
+            inv_fsq = stats.tile([P, 1], F32)
+            nc.gpsimd.tensor_tensor(out=inv_fsq[:], in0=inv_fnorm[:], in1=inv_fnorm[:], op=ALU.mult)
+            feat_t_of[blk] = feat_t
+            inv_fnorm_of[blk] = inv_fnorm
+            inv_fsq_of[blk] = inv_fsq
+
+        def multiply(blk):
+            chunk, r = divmod(blk, BLOCKS_PER_CHUNK)
+            ms = work.tile([P, C], F32)
+            for h in range(C // BANK):
+                acc = psum_m.tile([P, BANK], F32)
+                for s in range(PASSES):
+                    pixels = slice(s * CHUNK + r * P, s * CHUNK + (r + 1) * P)
+                    channels = slice(s * C + h * BANK, s * C + (h + 1) * BANK)
+                    nc.tensor.matmul_mx(
+                        out=acc[:],
+                        lhsT=codes_of[chunk][:, pixels].bitcast(E5M2_X4),
+                        lhsT_scale=scales_of[chunk][:, pixels],
+                        rhs=prot_codes[:, channels].bitcast(E4M3_X4),
+                        rhs_scale=prot_scales[:, channels],
+                        start=(s == 0),
+                        stop=(s == PASSES - 1),
+                    )
+                nc.scalar.activation(
+                    out=ms[:, h * BANK : (h + 1) * BANK], in_=acc[:], func=ACT.Copy, scale=inv_fnorm_of[blk][:, 0:1]
+                )
+            ms_of[blk] = ms
+
+        def project(blk):
+            products = unread.tile([P, C], F32)
+            coef = stats.tile([P, 1], F32)
+            nc.vector.scalar_tensor_tensor(
+                out=products[:],
+                in0=feat_t_of[blk][:],
+                scalar=inv_fsq_of[blk][:, 0:1],
+                in1=ms_of[blk][:],
+                op0=ALU.mult,
+                op1=ALU.mult,
+                accum_out=coef[:],
+            )
+            neg_res = work.tile([P, C], F32)
+            nc.vector.scalar_tensor_tensor(
+                out=neg_res[:],
+                in0=feat_t_of[blk][:],
+                scalar=coef[:, 0:1],
+                in1=ms_of[blk][:],
+                op0=ALU.mult,
+                op1=ALU.subtract,
+            )
+            neg_res_of[blk] = neg_res
+
+        def transpose_result(blk):
+            chunk, r = divmod(blk, BLOCKS_PER_CHUNK)
+            b, part = divmod(chunk, CHUNKS_PER_BATCH)
+            if r == 0:
+                out_sb = stores.tile([P, C_TILES, CHUNK], F32)
+                out_sb_of[chunk] = out_sb
+            per_bank = BANK // P
+            for h in range(C_TILES // per_bank):
+                flipped = psum_out.tile([P, BANK], F32)
+                for i in range(per_bank):
+                    c_tile = h * per_bank + i
+                    nc.tensor.transpose(
+                        out=flipped[:, i * P : (i + 1) * P],
+                        in_=neg_res_of[blk][:, c_tile * P : (c_tile + 1) * P],
+                        identity=ident_f32[:],
+                    )
+                nc.scalar.activation(
+                    out=out_sb_of[chunk][:, h * per_bank : (h + 1) * per_bank, r * P : (r + 1) * P],
+                    in_=flipped[:].rearrange("p (i n) -> p i n", i=per_bank),
+                    func=ACT.Copy,
+                    scale=-1.0,
+                )
+            if r == BLOCKS_PER_CHUNK - 1:
+                nc.scalar.dma_start(
+                    out=out_dram[b][:, :, part * CHUNK : (part + 1) * CHUNK], in_=out_sb_of[chunk][:]
+                )
+
+        for step in range(BLOCKS + 3):
+            if step < BLOCKS:
+                transpose_features(step)
+            if step == 0:
+                quantise_grad(0)
+            if 0 <= step - 1 < BLOCKS:
+                multiply(step - 1)
+            if 0 <= step - 2 < BLOCKS:
+                project(step - 2)
+            next_chunk, quarter = divmod(step, BLOCKS_PER_CHUNK)
+            next_chunk += 1
+            if next_chunk < BLOCKS // BLOCKS_PER_CHUNK:
+                if quarter == 0:
+                    scale_grad(next_chunk, 0)
+                if quarter == 1:
+                    scale_grad(next_chunk, 1)
+                    regroup_grad(next_chunk, 0)
+                if quarter == 2:
+                    regroup_grad(next_chunk, 1)
+                if quarter == 3:
+                    quantise_grad(next_chunk)
+            if 0 <= step - 3:
+                transpose_result(step - 3)
+            b, q = divmod(step, BLOCKS_PER_BATCH)
+            if b + 2 < B and q == 2:
+                load_grad(b + 2)
+            if b + 2 < B and q == BLOCKS_PER_BATCH - 1:
+                load_features(b + 2)

@@ -23,6 +23,10 @@ BLOCKS_PER_BATCH = N // P
 CHUNK = 512
 BLOCKS_PER_CHUNK = CHUNK // P
 CHUNKS_PER_BATCH = N // CHUNK
+CHUNKS = B * CHUNKS_PER_BATCH
+CHUNKS_AHEAD = 2
+STORE = 256
+BLOCKS_PER_STORE = STORE // P
 
 FLOPS = 2 * B * N * K * C
 
@@ -42,8 +46,8 @@ def tile_globalprototype_t_kernel(tc, features, prototypes, grad_out, out):
         work = stack.enter_context(tc.tile_pool(name="work", bufs=3))
         unread = stack.enter_context(tc.tile_pool(name="unread", bufs=2))
         stats = stack.enter_context(tc.tile_pool(name="stats", bufs=6))
-        stores = stack.enter_context(tc.tile_pool(name="stores", bufs=2))
-        psum_ft = stack.enter_context(tc.psum_pool(name="psum_ft", bufs=3))
+        stores = stack.enter_context(tc.tile_pool(name="stores", bufs=3))
+        psum_ft = stack.enter_context(tc.psum_pool(name="psum_ft", bufs=4))
         psum_m = stack.enter_context(tc.psum_pool(name="psum_m", bufs=2))
         psum_out = stack.enter_context(tc.psum_pool(name="psum_out", bufs=2))
         stack.enter_context(tc.manual_schedule())
@@ -102,54 +106,42 @@ def tile_globalprototype_t_kernel(tc, features, prototypes, grad_out, out):
                 in_=prot_grouped[s][:],
             )
 
-        def invert_norms(s, pnorm_sq):
+        for s in range(PASSES):
+            pnorm_sq = const.tile([P, PACK], F32, name="pnorm_sq%d" % s)
+            for j in range(PACK):
+                squares = unread.tile([P, C], BF16)
+                nc.scalar.activation(
+                    out=squares[:], in_=prot_of[s][:, j, :], func=ACT.Square, accum_out=pnorm_sq[:, j : j + 1]
+                )
             inv = const.tile([P, PACK], F32, name="inv_pnorm%d" % s)
             nc.gpsimd.tensor_tensor(out=inv[:], in0=pnorm_sq[:], in1=minus_half[:], op=ALU.pow)
             inv_pnorm[s] = inv
-
-        pnorm_sq0 = const.tile([P, PACK], F32)
-        for j in range(PACK):
-            squares = unread.tile([P, C], BF16)
-            nc.scalar.activation(
-                out=squares[:], in_=prot_of[0][:, j, :], func=ACT.Square, accum_out=pnorm_sq0[:, j : j + 1]
-            )
-        invert_norms(0, pnorm_sq0)
-
         regroup_prototypes(0)
-        pnorm_sq1 = const.tile([P, PACK], F32)
-        for j in range(PACK):
-            products = unread.tile([P, C], F32)
-            nc.vector.scalar_tensor_tensor(
-                out=products[:],
-                in0=prot_of[1][:, j, :],
-                scalar=1.0,
-                in1=prot_of[1][:, j, :],
-                op0=ALU.mult,
-                op1=ALU.mult,
-                accum_out=pnorm_sq1[:, j : j + 1],
-            )
-        invert_norms(1, pnorm_sq1)
-        quantise_prototypes(0)
         regroup_prototypes(1)
+        quantise_prototypes(0)
+        quantise_prototypes(1)
 
         scaled_of = {}
         grouped_of = {}
         codes_of = {}
         scales_of = {}
 
-        def scale_grad(chunk, s):
+        def scale_grad(chunk, s, engine):
             b, part = divmod(chunk, CHUNKS_PER_BATCH)
             if s == 0:
                 scaled = quant.tile([P, PASSES, PACK, CHUNK], BF16)
                 scaled_of[chunk] = scaled
             for j in range(PACK):
-                nc.vector.tensor_scalar(
+                engine.tensor_scalar(
                     out=scaled_of[chunk][:, s, j, :],
                     in0=grad_of[b][:, s, j, part * CHUNK : (part + 1) * CHUNK],
                     scalar1=inv_pnorm[s][:, j : j + 1],
-                    scalar2=None,
+                    scalar2=0.0,
                     op0=ALU.mult,
+                    op1=ALU.add,
                 )
+            if part == CHUNKS_PER_BATCH - 1 and s == PASSES - 1 and b + 2 < B:
+                load_grad(b + 2)
 
         def regroup_grad(chunk, s):
             if s == 0:
@@ -159,17 +151,22 @@ def tile_globalprototype_t_kernel(tc, features, prototypes, grad_out, out):
             regroup(by_pass[:, s], scaled_of[chunk][:, s])
 
         def quantise_grad(chunk):
-            codes = quant.tile([P, PASSES * CHUNK], U32, align_bytes=64)
-            scales = quant.tile([P, PASSES * CHUNK], U8, align_bytes=64)
+            codes = quant.tile([P, PASSES * CHUNK], U32, align_bytes=64, bufs=CHUNKS_AHEAD + 1)
+            scales = quant.tile([P, PASSES * CHUNK], U8, align_bytes=64, bufs=CHUNKS_AHEAD + 1)
             nc.vector.quantize_mx(out=codes[:].bitcast(E5M2_X4), scales=scales[:], in_=grouped_of[chunk][:])
             codes_of[chunk] = codes
             scales_of[chunk] = scales
 
-        scale_grad(0, 0)
-        quantise_prototypes(1)
-        scale_grad(0, 1)
+        scale_grad(0, 0, nc.vector)
         regroup_grad(0, 0)
+        scale_grad(1, 0, nc.vector)
+        regroup_grad(1, 0)
+        scale_grad(0, 1, nc.vector)
         regroup_grad(0, 1)
+        scale_grad(1, 1, nc.vector)
+        quantise_grad(0)
+        regroup_grad(1, 1)
+        quantise_grad(1)
 
         feat_t_of = {}
         inv_fnorm_of = {}
@@ -220,7 +217,9 @@ def tile_globalprototype_t_kernel(tc, features, prototypes, grad_out, out):
                 )
             ms_of[blk] = ms
 
-        def project(blk):
+        coef_of = {}
+
+        def projection_coefficient(blk):
             products = unread.tile([P, C], F32)
             coef = stats.tile([P, 1], F32)
             nc.vector.scalar_tensor_tensor(
@@ -232,11 +231,14 @@ def tile_globalprototype_t_kernel(tc, features, prototypes, grad_out, out):
                 op1=ALU.mult,
                 accum_out=coef[:],
             )
+            coef_of[blk] = coef
+
+        def subtract_projection(blk):
             neg_res = work.tile([P, C], F32)
             nc.vector.scalar_tensor_tensor(
                 out=neg_res[:],
                 in0=feat_t_of[blk][:],
-                scalar=coef[:, 0:1],
+                scalar=coef_of[blk][:, 0:1],
                 in1=ms_of[blk][:],
                 op0=ALU.mult,
                 op1=ALU.subtract,
@@ -244,11 +246,11 @@ def tile_globalprototype_t_kernel(tc, features, prototypes, grad_out, out):
             neg_res_of[blk] = neg_res
 
         def transpose_result(blk):
-            chunk, r = divmod(blk, BLOCKS_PER_CHUNK)
-            b, part = divmod(chunk, CHUNKS_PER_BATCH)
+            store, r = divmod(blk, BLOCKS_PER_STORE)
+            b, part = divmod(store, N // STORE)
             if r == 0:
-                out_sb = stores.tile([P, C_TILES, CHUNK], F32)
-                out_sb_of[chunk] = out_sb
+                out_sb = stores.tile([P, C_TILES, STORE], F32)
+                out_sb_of[store] = out_sb
             per_bank = BANK // P
             for h in range(C_TILES // per_bank):
                 flipped = psum_out.tile([P, BANK], F32)
@@ -259,42 +261,40 @@ def tile_globalprototype_t_kernel(tc, features, prototypes, grad_out, out):
                         in_=neg_res_of[blk][:, c_tile * P : (c_tile + 1) * P],
                         identity=ident_f32[:],
                     )
-                nc.scalar.activation(
-                    out=out_sb_of[chunk][:, h * per_bank : (h + 1) * per_bank, r * P : (r + 1) * P],
-                    in_=flipped[:].rearrange("p (i n) -> p i n", i=per_bank),
-                    func=ACT.Copy,
-                    scale=-1.0,
-                )
-            if r == BLOCKS_PER_CHUNK - 1:
-                nc.scalar.dma_start(
-                    out=out_dram[b][:, :, part * CHUNK : (part + 1) * CHUNK], in_=out_sb_of[chunk][:]
+                result = out_sb_of[store][:, h * per_bank : (h + 1) * per_bank, r * P : (r + 1) * P]
+                by_tile = flipped[:].rearrange("p (i n) -> p i n", i=per_bank)
+                if blk % 2 == 1 and h == 1:
+                    nc.vector.tensor_scalar(out=result, in0=by_tile, scalar1=-1.0, scalar2=None, op0=ALU.mult)
+                else:
+                    nc.scalar.activation(out=result, in_=by_tile, func=ACT.Copy, scale=-1.0)
+            if r == BLOCKS_PER_STORE - 1:
+                nc.sync.dma_start(
+                    out=out_dram[b][:, :, part * STORE : (part + 1) * STORE], in_=out_sb_of[store][:]
                 )
 
         for step in range(BLOCKS + 3):
             if step < BLOCKS:
                 transpose_features(step)
-            if step == 0:
-                quantise_grad(0)
             if 0 <= step - 1 < BLOCKS:
                 multiply(step - 1)
             if 0 <= step - 2 < BLOCKS:
-                project(step - 2)
-            next_chunk, quarter = divmod(step, BLOCKS_PER_CHUNK)
-            next_chunk += 1
-            if next_chunk < BLOCKS // BLOCKS_PER_CHUNK:
+                projection_coefficient(step - 2)
+            chunk_now, quarter = divmod(step, BLOCKS_PER_CHUNK)
+            next_chunk = chunk_now + CHUNKS_AHEAD
+            if next_chunk < CHUNKS:
                 if quarter == 0:
-                    scale_grad(next_chunk, 0)
+                    scale_grad(next_chunk, 0, nc.gpsimd)
                 if quarter == 1:
-                    scale_grad(next_chunk, 1)
+                    scale_grad(next_chunk, 1, nc.gpsimd)
                     regroup_grad(next_chunk, 0)
                 if quarter == 2:
                     regroup_grad(next_chunk, 1)
                 if quarter == 3:
                     quantise_grad(next_chunk)
+            if 0 <= step - 2 < BLOCKS:
+                subtract_projection(step - 2)
             if 0 <= step - 3:
                 transpose_result(step - 3)
             b, q = divmod(step, BLOCKS_PER_BATCH)
-            if b + 2 < B and q == 2:
-                load_grad(b + 2)
             if b + 2 < B and q == BLOCKS_PER_BATCH - 1:
                 load_features(b + 2)

@@ -126,19 +126,18 @@ def tile_globalprototype_t_kernel(tc, features, prototypes, grad_out, out):
         codes_of = {}
         scales_of = {}
 
-        def scale_grad(chunk, s, engine):
+        def scale_grad(chunk, s):
             b, part = divmod(chunk, CHUNKS_PER_BATCH)
             if s == 0:
                 scaled = quant.tile([P, PASSES, PACK, CHUNK], BF16)
                 scaled_of[chunk] = scaled
             for j in range(PACK):
-                engine.tensor_scalar(
+                nc.vector.tensor_scalar(
                     out=scaled_of[chunk][:, s, j, :],
                     in0=grad_of[b][:, s, j, part * CHUNK : (part + 1) * CHUNK],
                     scalar1=inv_pnorm[s][:, j : j + 1],
-                    scalar2=0.0,
+                    scalar2=None,
                     op0=ALU.mult,
-                    op1=ALU.add,
                 )
             if part == CHUNKS_PER_BATCH - 1 and s == PASSES - 1 and b + 2 < B:
                 load_grad(b + 2)
@@ -157,13 +156,13 @@ def tile_globalprototype_t_kernel(tc, features, prototypes, grad_out, out):
             codes_of[chunk] = codes
             scales_of[chunk] = scales
 
-        scale_grad(0, 0, nc.vector)
+        scale_grad(0, 0)
         regroup_grad(0, 0)
-        scale_grad(1, 0, nc.vector)
+        scale_grad(1, 0)
         regroup_grad(1, 0)
-        scale_grad(0, 1, nc.vector)
+        scale_grad(0, 1)
         regroup_grad(0, 1)
-        scale_grad(1, 1, nc.vector)
+        scale_grad(1, 1)
         quantise_grad(0)
         regroup_grad(1, 1)
         quantise_grad(1)
@@ -217,9 +216,7 @@ def tile_globalprototype_t_kernel(tc, features, prototypes, grad_out, out):
                 )
             ms_of[blk] = ms
 
-        coef_of = {}
-
-        def projection_coefficient(blk):
+        def project(blk):
             products = unread.tile([P, C], F32)
             coef = stats.tile([P, 1], F32)
             nc.vector.scalar_tensor_tensor(
@@ -231,14 +228,11 @@ def tile_globalprototype_t_kernel(tc, features, prototypes, grad_out, out):
                 op1=ALU.mult,
                 accum_out=coef[:],
             )
-            coef_of[blk] = coef
-
-        def subtract_projection(blk):
             neg_res = work.tile([P, C], F32)
             nc.vector.scalar_tensor_tensor(
                 out=neg_res[:],
                 in0=feat_t_of[blk][:],
-                scalar=coef_of[blk][:, 0:1],
+                scalar=coef[:, 0:1],
                 in1=ms_of[blk][:],
                 op0=ALU.mult,
                 op1=ALU.subtract,
@@ -261,12 +255,12 @@ def tile_globalprototype_t_kernel(tc, features, prototypes, grad_out, out):
                         in_=neg_res_of[blk][:, c_tile * P : (c_tile + 1) * P],
                         identity=ident_f32[:],
                     )
-                result = out_sb_of[store][:, h * per_bank : (h + 1) * per_bank, r * P : (r + 1) * P]
-                by_tile = flipped[:].rearrange("p (i n) -> p i n", i=per_bank)
-                if blk % 2 == 1 and h == 1:
-                    nc.vector.tensor_scalar(out=result, in0=by_tile, scalar1=-1.0, scalar2=None, op0=ALU.mult)
-                else:
-                    nc.scalar.activation(out=result, in_=by_tile, func=ACT.Copy, scale=-1.0)
+                nc.scalar.activation(
+                    out=out_sb_of[store][:, h * per_bank : (h + 1) * per_bank, r * P : (r + 1) * P],
+                    in_=flipped[:].rearrange("p (i n) -> p i n", i=per_bank),
+                    func=ACT.Copy,
+                    scale=-1.0,
+                )
             if r == BLOCKS_PER_STORE - 1:
                 nc.sync.dma_start(
                     out=out_dram[b][:, :, part * STORE : (part + 1) * STORE], in_=out_sb_of[store][:]
@@ -278,21 +272,19 @@ def tile_globalprototype_t_kernel(tc, features, prototypes, grad_out, out):
             if 0 <= step - 1 < BLOCKS:
                 multiply(step - 1)
             if 0 <= step - 2 < BLOCKS:
-                projection_coefficient(step - 2)
+                project(step - 2)
             chunk_now, quarter = divmod(step, BLOCKS_PER_CHUNK)
             next_chunk = chunk_now + CHUNKS_AHEAD
             if next_chunk < CHUNKS:
                 if quarter == 0:
-                    scale_grad(next_chunk, 0, nc.gpsimd)
+                    scale_grad(next_chunk, 0)
                 if quarter == 1:
-                    scale_grad(next_chunk, 1, nc.gpsimd)
+                    scale_grad(next_chunk, 1)
                     regroup_grad(next_chunk, 0)
                 if quarter == 2:
                     regroup_grad(next_chunk, 1)
                 if quarter == 3:
                     quantise_grad(next_chunk)
-            if 0 <= step - 2 < BLOCKS:
-                subtract_projection(step - 2)
             if 0 <= step - 3:
                 transpose_result(step - 3)
             b, q = divmod(step, BLOCKS_PER_BATCH)

@@ -27,6 +27,8 @@ CHUNKS = B * CHUNKS_PER_BATCH
 CHUNKS_AHEAD = 2
 STORE = 256
 BLOCKS_PER_STORE = STORE // P
+HALVES = C // BANK
+TILES_PER_HALF = BANK // P
 
 FLOPS = 2 * B * N * K * C
 
@@ -174,15 +176,20 @@ def tile_globalprototype_t_kernel(tc, features, prototypes, grad_out, out):
         neg_res_of = {}
         out_sb_of = {}
 
-        def transpose_features(blk):
+        def transpose_features(blk, h):
             b, q = divmod(blk, BLOCKS_PER_BATCH)
-            feat_t = psum_ft.tile([P, C], BF16)
-            for i in range(C_TILES):
+            if h == 0:
+                new_bank = psum_ft.tile([P, C], BF16)
+                feat_t_of[blk] = new_bank
+            feat_t = feat_t_of[blk]
+            for i in range(h * TILES_PER_HALF, (h + 1) * TILES_PER_HALF):
                 nc.tensor.transpose(
                     out=feat_t[:, i * P : (i + 1) * P],
                     in_=feat_of[b][:, i, q * P : (q + 1) * P],
                     identity=ident_bf16[:],
                 )
+            if h < HALVES - 1:
+                return
             squares = unread.tile([P, C], BF16)
             fnorm_sq = stats.tile([P, 1], F32)
             nc.scalar.activation(out=squares[:], in_=feat_t[:], func=ACT.Square, accum_out=fnorm_sq[:])
@@ -190,31 +197,33 @@ def tile_globalprototype_t_kernel(tc, features, prototypes, grad_out, out):
             nc.gpsimd.tensor_tensor(out=inv_fnorm[:], in0=fnorm_sq[:], in1=minus_half[:, 0:1], op=ALU.pow)
             inv_fsq = stats.tile([P, 1], F32)
             nc.gpsimd.tensor_tensor(out=inv_fsq[:], in0=inv_fnorm[:], in1=inv_fnorm[:], op=ALU.mult)
-            feat_t_of[blk] = feat_t
             inv_fnorm_of[blk] = inv_fnorm
             inv_fsq_of[blk] = inv_fsq
 
-        def multiply(blk):
+        def multiply(blk, h):
             chunk, r = divmod(blk, BLOCKS_PER_CHUNK)
-            ms = work.tile([P, C], F32)
-            for h in range(C // BANK):
-                acc = psum_m.tile([P, BANK], F32)
-                for s in range(PASSES):
-                    pixels = slice(s * CHUNK + r * P, s * CHUNK + (r + 1) * P)
-                    channels = slice(s * C + h * BANK, s * C + (h + 1) * BANK)
-                    nc.tensor.matmul_mx(
-                        out=acc[:],
-                        lhsT=codes_of[chunk][:, pixels].bitcast(E5M2_X4),
-                        lhsT_scale=scales_of[chunk][:, pixels],
-                        rhs=prot_codes[:, channels].bitcast(E4M3_X4),
-                        rhs_scale=prot_scales[:, channels],
-                        start=(s == 0),
-                        stop=(s == PASSES - 1),
-                    )
-                nc.scalar.activation(
-                    out=ms[:, h * BANK : (h + 1) * BANK], in_=acc[:], func=ACT.Copy, scale=inv_fnorm_of[blk][:, 0:1]
+            if h == 0:
+                ms = work.tile([P, C], F32)
+                ms_of[blk] = ms
+            acc = psum_m.tile([P, BANK], F32)
+            for s in range(PASSES):
+                pixels = slice(s * CHUNK + r * P, s * CHUNK + (r + 1) * P)
+                channels = slice(s * C + h * BANK, s * C + (h + 1) * BANK)
+                nc.tensor.matmul_mx(
+                    out=acc[:],
+                    lhsT=codes_of[chunk][:, pixels].bitcast(E5M2_X4),
+                    lhsT_scale=scales_of[chunk][:, pixels],
+                    rhs=prot_codes[:, channels].bitcast(E4M3_X4),
+                    rhs_scale=prot_scales[:, channels],
+                    start=(s == 0),
+                    stop=(s == PASSES - 1),
                 )
-            ms_of[blk] = ms
+            nc.scalar.activation(
+                out=ms_of[blk][:, h * BANK : (h + 1) * BANK],
+                in_=acc[:],
+                func=ACT.Copy,
+                scale=inv_fnorm_of[blk][:, 0:1],
+            )
 
         def project(blk):
             products = unread.tile([P, C], F32)
@@ -239,38 +248,39 @@ def tile_globalprototype_t_kernel(tc, features, prototypes, grad_out, out):
             )
             neg_res_of[blk] = neg_res
 
-        def transpose_result(blk):
+        def transpose_result(blk, h):
             store, r = divmod(blk, BLOCKS_PER_STORE)
             b, part = divmod(store, N // STORE)
-            if r == 0:
+            if r == 0 and h == 0:
                 out_sb = stores.tile([P, C_TILES, STORE], F32)
                 out_sb_of[store] = out_sb
-            per_bank = BANK // P
-            for h in range(C_TILES // per_bank):
-                flipped = psum_out.tile([P, BANK], F32)
-                for i in range(per_bank):
-                    c_tile = h * per_bank + i
-                    nc.tensor.transpose(
-                        out=flipped[:, i * P : (i + 1) * P],
-                        in_=neg_res_of[blk][:, c_tile * P : (c_tile + 1) * P],
-                        identity=ident_f32[:],
-                    )
-                nc.scalar.activation(
-                    out=out_sb_of[store][:, h * per_bank : (h + 1) * per_bank, r * P : (r + 1) * P],
-                    in_=flipped[:].rearrange("p (i n) -> p i n", i=per_bank),
-                    func=ACT.Copy,
-                    scale=-1.0,
+            flipped = psum_out.tile([P, BANK], F32)
+            for i in range(TILES_PER_HALF):
+                c_tile = h * TILES_PER_HALF + i
+                nc.tensor.transpose(
+                    out=flipped[:, i * P : (i + 1) * P],
+                    in_=neg_res_of[blk][:, c_tile * P : (c_tile + 1) * P],
+                    identity=ident_f32[:],
                 )
-            if r == BLOCKS_PER_STORE - 1:
+            nc.scalar.activation(
+                out=out_sb_of[store][:, h * TILES_PER_HALF : (h + 1) * TILES_PER_HALF, r * P : (r + 1) * P],
+                in_=flipped[:].rearrange("p (i n) -> p i n", i=TILES_PER_HALF),
+                func=ACT.Copy,
+                scale=-1.0,
+            )
+            if r == BLOCKS_PER_STORE - 1 and h == HALVES - 1:
                 nc.sync.dma_start(
                     out=out_dram[b][:, :, part * STORE : (part + 1) * STORE], in_=out_sb_of[store][:]
                 )
 
         for step in range(BLOCKS + 3):
-            if step < BLOCKS:
-                transpose_features(step)
-            if 0 <= step - 1 < BLOCKS:
-                multiply(step - 1)
+            for h in range(HALVES):
+                if step < BLOCKS:
+                    transpose_features(step, h)
+                if 0 <= step - 1 < BLOCKS:
+                    multiply(step - 1, h)
+                if 0 <= step - 3:
+                    transpose_result(step - 3, h)
             if 0 <= step - 2 < BLOCKS:
                 project(step - 2)
             chunk_now, quarter = divmod(step, BLOCKS_PER_CHUNK)
@@ -285,8 +295,6 @@ def tile_globalprototype_t_kernel(tc, features, prototypes, grad_out, out):
                     regroup_grad(next_chunk, 1)
                 if quarter == 3:
                     quantise_grad(next_chunk)
-            if 0 <= step - 3:
-                transpose_result(step - 3)
             b, q = divmod(step, BLOCKS_PER_BATCH)
             if b + 2 < B and q == BLOCKS_PER_BATCH - 1:
                 load_features(b + 2)

@@ -27,8 +27,6 @@ CHUNKS = B * CHUNKS_PER_BATCH
 CHUNKS_AHEAD = 2
 STORE = 256
 BLOCKS_PER_STORE = STORE // P
-HALVES = C // BANK
-TILES_PER_HALF = BANK // P
 
 FLOPS = 2 * B * N * K * C
 
@@ -78,7 +76,8 @@ def tile_globalprototype_t_kernel(tc, features, prototypes, grad_out, out):
         prot_of = {}
         for s in range(PASSES):
             prot_sb = const.tile([P, PACK, C], BF16, name="prot_sb%d" % s)
-            nc.sync.dma_start(out=prot_sb[:], in_=prot_dram[s])
+            for rows in (slice(0, PACK // 2), slice(PACK // 2, PACK)):
+                nc.sync.dma_start(out=prot_sb[:, rows], in_=prot_dram[s][:, rows])
             prot_of[s] = prot_sb
         for b in range(2):
             load_grad(b)
@@ -176,20 +175,15 @@ def tile_globalprototype_t_kernel(tc, features, prototypes, grad_out, out):
         neg_res_of = {}
         out_sb_of = {}
 
-        def transpose_features(blk, h):
+        def transpose_features(blk):
             b, q = divmod(blk, BLOCKS_PER_BATCH)
-            if h == 0:
-                new_bank = psum_ft.tile([P, C], BF16)
-                feat_t_of[blk] = new_bank
-            feat_t = feat_t_of[blk]
-            for i in range(h * TILES_PER_HALF, (h + 1) * TILES_PER_HALF):
+            feat_t = psum_ft.tile([P, C], BF16)
+            for i in range(C_TILES):
                 nc.tensor.transpose(
                     out=feat_t[:, i * P : (i + 1) * P],
                     in_=feat_of[b][:, i, q * P : (q + 1) * P],
                     identity=ident_bf16[:],
                 )
-            if h < HALVES - 1:
-                return
             squares = unread.tile([P, C], BF16)
             fnorm_sq = stats.tile([P, 1], F32)
             nc.scalar.activation(out=squares[:], in_=feat_t[:], func=ACT.Square, accum_out=fnorm_sq[:])
@@ -197,35 +191,35 @@ def tile_globalprototype_t_kernel(tc, features, prototypes, grad_out, out):
             nc.gpsimd.tensor_tensor(out=inv_fnorm[:], in0=fnorm_sq[:], in1=minus_half[:, 0:1], op=ALU.pow)
             inv_fsq = stats.tile([P, 1], F32)
             nc.gpsimd.tensor_tensor(out=inv_fsq[:], in0=inv_fnorm[:], in1=inv_fnorm[:], op=ALU.mult)
+            feat_t_of[blk] = feat_t
             inv_fnorm_of[blk] = inv_fnorm
             inv_fsq_of[blk] = inv_fsq
 
-        def multiply(blk, h):
+        def multiply(blk):
             chunk, r = divmod(blk, BLOCKS_PER_CHUNK)
-            if h == 0:
-                ms = work.tile([P, C], F32)
-                ms_of[blk] = ms
-            acc = psum_m.tile([P, BANK], F32)
-            for s in range(PASSES):
-                pixels = slice(s * CHUNK + r * P, s * CHUNK + (r + 1) * P)
-                channels = slice(s * C + h * BANK, s * C + (h + 1) * BANK)
-                nc.tensor.matmul_mx(
-                    out=acc[:],
-                    lhsT=codes_of[chunk][:, pixels].bitcast(E5M2_X4),
-                    lhsT_scale=scales_of[chunk][:, pixels],
-                    rhs=prot_codes[:, channels].bitcast(E4M3_X4),
-                    rhs_scale=prot_scales[:, channels],
-                    start=(s == 0),
-                    stop=(s == PASSES - 1),
+            ms = work.tile([P, C], F32)
+            for h in range(C // BANK):
+                acc = psum_m.tile([P, BANK], F32)
+                for s in range(PASSES):
+                    pixels = slice(s * CHUNK + r * P, s * CHUNK + (r + 1) * P)
+                    channels = slice(s * C + h * BANK, s * C + (h + 1) * BANK)
+                    nc.tensor.matmul_mx(
+                        out=acc[:],
+                        lhsT=codes_of[chunk][:, pixels].bitcast(E5M2_X4),
+                        lhsT_scale=scales_of[chunk][:, pixels],
+                        rhs=prot_codes[:, channels].bitcast(E4M3_X4),
+                        rhs_scale=prot_scales[:, channels],
+                        start=(s == 0),
+                        stop=(s == PASSES - 1),
+                    )
+                nc.scalar.activation(
+                    out=ms[:, h * BANK : (h + 1) * BANK], in_=acc[:], func=ACT.Copy, scale=inv_fnorm_of[blk][:, 0:1]
                 )
-            nc.scalar.activation(
-                out=ms_of[blk][:, h * BANK : (h + 1) * BANK],
-                in_=acc[:],
-                func=ACT.Copy,
-                scale=inv_fnorm_of[blk][:, 0:1],
-            )
+            ms_of[blk] = ms
 
-        def project(blk):
+        coef_of = {}
+
+        def projection_coefficient(blk):
             products = unread.tile([P, C], F32)
             coef = stats.tile([P, 1], F32)
             nc.vector.scalar_tensor_tensor(
@@ -237,52 +231,54 @@ def tile_globalprototype_t_kernel(tc, features, prototypes, grad_out, out):
                 op1=ALU.mult,
                 accum_out=coef[:],
             )
+            coef_of[blk] = coef
+
+        def subtract_projection(blk):
             neg_res = work.tile([P, C], F32)
             nc.vector.scalar_tensor_tensor(
                 out=neg_res[:],
                 in0=feat_t_of[blk][:],
-                scalar=coef[:, 0:1],
+                scalar=coef_of[blk][:, 0:1],
                 in1=ms_of[blk][:],
                 op0=ALU.mult,
                 op1=ALU.subtract,
             )
             neg_res_of[blk] = neg_res
 
-        def transpose_result(blk, h):
+        def transpose_result(blk):
             store, r = divmod(blk, BLOCKS_PER_STORE)
             b, part = divmod(store, N // STORE)
-            if r == 0 and h == 0:
+            if r == 0:
                 out_sb = stores.tile([P, C_TILES, STORE], F32)
                 out_sb_of[store] = out_sb
-            flipped = psum_out.tile([P, BANK], F32)
-            for i in range(TILES_PER_HALF):
-                c_tile = h * TILES_PER_HALF + i
-                nc.tensor.transpose(
-                    out=flipped[:, i * P : (i + 1) * P],
-                    in_=neg_res_of[blk][:, c_tile * P : (c_tile + 1) * P],
-                    identity=ident_f32[:],
+            per_bank = BANK // P
+            for h in range(C_TILES // per_bank):
+                flipped = psum_out.tile([P, BANK], F32)
+                for i in range(per_bank):
+                    c_tile = h * per_bank + i
+                    nc.tensor.transpose(
+                        out=flipped[:, i * P : (i + 1) * P],
+                        in_=neg_res_of[blk][:, c_tile * P : (c_tile + 1) * P],
+                        identity=ident_f32[:],
+                    )
+                nc.scalar.activation(
+                    out=out_sb_of[store][:, h * per_bank : (h + 1) * per_bank, r * P : (r + 1) * P],
+                    in_=flipped[:].rearrange("p (i n) -> p i n", i=per_bank),
+                    func=ACT.Copy,
+                    scale=-1.0,
                 )
-            nc.scalar.activation(
-                out=out_sb_of[store][:, h * TILES_PER_HALF : (h + 1) * TILES_PER_HALF, r * P : (r + 1) * P],
-                in_=flipped[:].rearrange("p (i n) -> p i n", i=TILES_PER_HALF),
-                func=ACT.Copy,
-                scale=-1.0,
-            )
-            if r == BLOCKS_PER_STORE - 1 and h == HALVES - 1:
+            if r == BLOCKS_PER_STORE - 1:
                 nc.sync.dma_start(
                     out=out_dram[b][:, :, part * STORE : (part + 1) * STORE], in_=out_sb_of[store][:]
                 )
 
         for step in range(BLOCKS + 3):
-            for h in range(HALVES):
-                if step < BLOCKS:
-                    transpose_features(step, h)
-                if 0 <= step - 1 < BLOCKS:
-                    multiply(step - 1, h)
-                if 0 <= step - 3:
-                    transpose_result(step - 3, h)
+            if step < BLOCKS:
+                transpose_features(step)
+            if 0 <= step - 1 < BLOCKS:
+                multiply(step - 1)
             if 0 <= step - 2 < BLOCKS:
-                project(step - 2)
+                projection_coefficient(step - 2)
             chunk_now, quarter = divmod(step, BLOCKS_PER_CHUNK)
             next_chunk = chunk_now + CHUNKS_AHEAD
             if next_chunk < CHUNKS:
@@ -295,6 +291,10 @@ def tile_globalprototype_t_kernel(tc, features, prototypes, grad_out, out):
                     regroup_grad(next_chunk, 1)
                 if quarter == 3:
                     quantise_grad(next_chunk)
+            if 0 <= step - 2 < BLOCKS:
+                subtract_projection(step - 2)
+            if 0 <= step - 3:
+                transpose_result(step - 3)
             b, q = divmod(step, BLOCKS_PER_BATCH)
             if b + 2 < B and q == BLOCKS_PER_BATCH - 1:
                 load_features(b + 2)

@@ -28,6 +28,16 @@ CHUNKS_AHEAD = 2
 STORE = 256
 BLOCKS_PER_STORE = STORE // P
 
+GS_PLAN = (
+    (0, "scale", (0,)),
+    (1, "scale", (1,)),
+    (1, "regroup", (0, 0)),
+    (2, "regroup", (0, 1)),
+    (3, "regroup", (1, 0)),
+    (4, "regroup", (1, 1)),
+    (6, "quantise", ()),
+)
+
 FLOPS = 2 * B * N * K * C
 
 
@@ -150,6 +160,21 @@ def tile_globalprototype_t_kernel(tc, features, prototypes, grad_out, out):
             by_pass = grouped_of[chunk][:].rearrange("p (s w t) -> p s w t", s=PASSES, t=PACK)
             regroup(by_pass[:, s], scaled_of[chunk][:, s])
 
+        def regroup_grad_on_gpsimd(chunk, s, half):
+            if s == 0 and half == 0:
+                grouped = quant.tile([P, PASSES * CHUNK * PACK], BF16, align_bytes=64)
+                grouped_of[chunk] = grouped
+            by_pass = grouped_of[chunk][:].rearrange("p (s w t) -> p s w t", s=PASSES, t=PACK)
+            cols = slice(half * (CHUNK // 2), (half + 1) * (CHUNK // 2))
+            nc.gpsimd.tensor_scalar(
+                out=by_pass[:, s, cols, :],
+                in0=scaled_of[chunk][:, s, :, cols].rearrange("p t w -> p w t"),
+                scalar1=1.0,
+                scalar2=0.0,
+                op0=ALU.mult,
+                op1=ALU.add,
+            )
+
         def quantise_grad(chunk):
             codes = quant.tile([P, PASSES * CHUNK], U32, align_bytes=64, bufs=CHUNKS_AHEAD + 1)
             scales = quant.tile([P, PASSES * CHUNK], U8, align_bytes=64, bufs=CHUNKS_AHEAD + 1)
@@ -245,15 +270,29 @@ def tile_globalprototype_t_kernel(tc, features, prototypes, grad_out, out):
             )
             neg_res_of[blk] = neg_res
 
+        per_bank = BANK // P
+        flipped_of = {}
+
+        def vector_empties(blk, h):
+            return blk % 2 == 1 and h == 1
+
+        def empty_result_bank(blk, h):
+            store, r = divmod(blk, BLOCKS_PER_STORE)
+            dst = out_sb_of[store][:, h * per_bank : (h + 1) * per_bank, r * P : (r + 1) * P]
+            src = flipped_of[(blk, h)][:].rearrange("p (i n) -> p i n", i=per_bank)
+            if vector_empties(blk, h):
+                nc.vector.tensor_scalar(out=dst, in0=src, scalar1=-1.0, scalar2=None, op0=ALU.mult)
+            else:
+                nc.scalar.activation(out=dst, in_=src, func=ACT.Copy, scale=-1.0)
+
         def transpose_result(blk):
             store, r = divmod(blk, BLOCKS_PER_STORE)
-            b, part = divmod(store, N // STORE)
             if r == 0:
                 out_sb = stores.tile([P, C_TILES, STORE], F32)
                 out_sb_of[store] = out_sb
-            per_bank = BANK // P
             for h in range(C_TILES // per_bank):
                 flipped = psum_out.tile([P, BANK], F32)
+                flipped_of[(blk, h)] = flipped
                 for i in range(per_bank):
                     c_tile = h * per_bank + i
                     nc.tensor.transpose(
@@ -261,39 +300,47 @@ def tile_globalprototype_t_kernel(tc, features, prototypes, grad_out, out):
                         in_=neg_res_of[blk][:, c_tile * P : (c_tile + 1) * P],
                         identity=ident_f32[:],
                     )
-                nc.scalar.activation(
-                    out=out_sb_of[store][:, h * per_bank : (h + 1) * per_bank, r * P : (r + 1) * P],
-                    in_=flipped[:].rearrange("p (i n) -> p i n", i=per_bank),
-                    func=ACT.Copy,
-                    scale=-1.0,
-                )
+                if not vector_empties(blk, h):
+                    empty_result_bank(blk, h)
+
+        def finish_result(blk):
+            store, r = divmod(blk, BLOCKS_PER_STORE)
+            b, part = divmod(store, N // STORE)
+            for h in range(C_TILES // per_bank):
+                if vector_empties(blk, h):
+                    empty_result_bank(blk, h)
             if r == BLOCKS_PER_STORE - 1:
                 nc.sync.dma_start(
                     out=out_dram[b][:, :, part * STORE : (part + 1) * STORE], in_=out_sb_of[store][:]
                 )
 
-        for step in range(BLOCKS + 3):
+        def gs_tasks(step, kind):
+            found = []
+            for chunk in range(CHUNKS_AHEAD, CHUNKS):
+                u = step - BLOCKS_PER_CHUNK * (chunk - CHUNKS_AHEAD)
+                for when, what, args in GS_PLAN:
+                    if when == u and what == kind:
+                        found.append((chunk,) + args)
+            return found
+
+        for step in range(BLOCKS + 4):
+            for chunk, s, half in gs_tasks(step, "regroup"):
+                regroup_grad_on_gpsimd(chunk, s, half)
+            if 0 <= step - 4:
+                finish_result(step - 4)
             if step < BLOCKS:
                 transpose_features(step)
             if 0 <= step - 1 < BLOCKS:
                 multiply(step - 1)
             if 0 <= step - 2 < BLOCKS:
                 projection_coefficient(step - 2)
-            chunk_now, quarter = divmod(step, BLOCKS_PER_CHUNK)
-            next_chunk = chunk_now + CHUNKS_AHEAD
-            if next_chunk < CHUNKS:
-                if quarter == 0:
-                    scale_grad(next_chunk, 0)
-                if quarter == 1:
-                    scale_grad(next_chunk, 1)
-                    regroup_grad(next_chunk, 0)
-                if quarter == 2:
-                    regroup_grad(next_chunk, 1)
-                if quarter == 3:
-                    quantise_grad(next_chunk)
+            for chunk, s in gs_tasks(step, "scale"):
+                scale_grad(chunk, s)
+            for (chunk,) in gs_tasks(step, "quantise"):
+                quantise_grad(chunk)
             if 0 <= step - 2 < BLOCKS:
                 subtract_projection(step - 2)
-            if 0 <= step - 3:
+            if 0 <= step - 3 < BLOCKS:
                 transpose_result(step - 3)
             b, q = divmod(step, BLOCKS_PER_BATCH)
             if b + 2 < B and q == BLOCKS_PER_BATCH - 1:

@@ -18,13 +18,14 @@ PACK = 4
 PASSES = K // (P * PACK)
 BANK = 512
 C_TILES = C // P
+C_HALVES = C // BANK
 BLOCKS = B * N // P
-BLOCKS_PER_BATCH = N // P
 CHUNK = 512
+HALF = CHUNK // 2
 BLOCKS_PER_CHUNK = CHUNK // P
 CHUNKS_PER_BATCH = N // CHUNK
 CHUNKS = B * CHUNKS_PER_BATCH
-CHUNKS_AHEAD = 2
+LOADS_AHEAD = 4
 STORE = 256
 BLOCKS_PER_STORE = STORE // P
 
@@ -37,6 +38,7 @@ GS_PLAN = (
     (4, "regroup", (1, 1)),
     (6, "quantise", ()),
 )
+FIRST_PLANNED_CHUNK = 2
 
 FLOPS = 2 * B * N * K * C
 
@@ -51,7 +53,7 @@ def tile_globalprototype_t_kernel(tc, features, prototypes, grad_out, out):
 
     with ExitStack() as stack:
         const = stack.enter_context(tc.tile_pool(name="const", bufs=1))
-        loads = stack.enter_context(tc.tile_pool(name="loads", bufs=2))
+        loads = stack.enter_context(tc.tile_pool(name="loads", bufs=LOADS_AHEAD))
         quant = stack.enter_context(tc.tile_pool(name="quant", bufs=2))
         work = stack.enter_context(tc.tile_pool(name="work", bufs=3))
         unread = stack.enter_context(tc.tile_pool(name="unread", bufs=2))
@@ -72,16 +74,22 @@ def tile_globalprototype_t_kernel(tc, features, prototypes, grad_out, out):
         grad_of = {}
         feat_of = {}
 
-        def load_grad(b):
-            grad_sb = loads.tile([P, PASSES, PACK, N], BF16)
-            for s in range(PASSES):
-                nc.sync.dma_start(out=grad_sb[:, s], in_=grad_dram[b, s])
-            grad_of[b] = grad_sb
+        def pixels_of(chunk):
+            b, part = divmod(chunk, CHUNKS_PER_BATCH)
+            return b, slice(part * CHUNK, (part + 1) * CHUNK)
 
-        def load_features(b):
-            feat_sb = loads.tile([P, C_TILES, N], BF16)
-            nc.sync.dma_start(out=feat_sb[:], in_=feat_dram[b])
-            feat_of[b] = feat_sb
+        def load_grad(chunk):
+            b, cols = pixels_of(chunk)
+            grad_sb = loads.tile([P, PASSES, PACK, CHUNK], BF16)
+            for s in range(PASSES):
+                nc.sync.dma_start(out=grad_sb[:, s], in_=grad_dram[b, s][:, :, cols])
+            grad_of[chunk] = grad_sb
+
+        def load_features(chunk):
+            b, cols = pixels_of(chunk)
+            feat_sb = loads.tile([P, C_TILES, CHUNK], BF16)
+            nc.sync.dma_start(out=feat_sb[:], in_=feat_dram[b][:, :, cols])
+            feat_of[chunk] = feat_sb
 
         prot_of = {}
         for s in range(PASSES):
@@ -89,48 +97,68 @@ def tile_globalprototype_t_kernel(tc, features, prototypes, grad_out, out):
             for rows in (slice(0, PACK // 2), slice(PACK // 2, PACK)):
                 nc.sync.dma_start(out=prot_sb[:, rows], in_=prot_dram[s][:, rows])
             prot_of[s] = prot_sb
-        for b in range(2):
-            load_grad(b)
-            load_features(b)
+        for chunk in range(LOADS_AHEAD):
+            load_grad(chunk)
+            load_features(chunk)
 
-        def regroup(grouped, rows):
+        def regroup_on_vector(grouped, rows):
             nc.vector.tensor_copy(
                 out=grouped.rearrange("p (c i) t -> p c t i", i=4),
                 in_=rows.rearrange("p t (c i) -> p c t i", i=4),
             )
 
+        def regroup_on_gpsimd(grouped, rows):
+            nc.gpsimd.tensor_scalar(
+                out=grouped,
+                in0=rows.rearrange("p t w -> p w t"),
+                scalar1=1.0,
+                scalar2=0.0,
+                op0=ALU.mult,
+                op1=ALU.add,
+            )
+
         prot_codes = const.tile([P, PASSES * C], U32, align_bytes=64)
         prot_scales = const.tile([P, PASSES * C], U8, align_bytes=64)
         prot_grouped = {}
+        pnorm_sq = {}
         inv_pnorm = {}
+        for s in range(PASSES):
+            prot_grouped[s] = const.tile([P, C * PACK], BF16, align_bytes=64, name="prot_grouped%d" % s)
+            pnorm_sq[s] = const.tile([P, PACK], F32, name="pnorm_sq%d" % s)
+            inv_pnorm[s] = const.tile([P, PACK], F32, name="inv_pnorm%d" % s)
 
-        def regroup_prototypes(s):
-            grouped = quant.tile([P, PACK * C], BF16, align_bytes=64)
-            regroup(grouped[:].rearrange("p (w t) -> p w t", t=PACK), prot_of[s][:])
-            prot_grouped[s] = grouped
+        def regroup_prototypes(s, h, regroup):
+            by_word = prot_grouped[s][:].rearrange("p (w t) -> p w t", t=PACK)
+            regroup(by_word[:, h * BANK : (h + 1) * BANK, :], prot_of[s][:, :, h * BANK : (h + 1) * BANK])
 
-        def quantise_prototypes(s):
-            cols = slice(s * C, (s + 1) * C)
+        def quantise_prototypes(s, h):
+            cols = slice(s * C + h * BANK, s * C + (h + 1) * BANK)
             nc.vector.quantize_mx(
                 out=prot_codes[:, cols].bitcast(E4M3_X4),
                 scales=prot_scales[:, cols],
-                in_=prot_grouped[s][:],
+                in_=prot_grouped[s][:, h * BANK * PACK : (h + 1) * BANK * PACK],
             )
 
-        for s in range(PASSES):
-            pnorm_sq = const.tile([P, PACK], F32, name="pnorm_sq%d" % s)
-            for j in range(PACK):
-                squares = unread.tile([P, C], BF16)
-                nc.scalar.activation(
-                    out=squares[:], in_=prot_of[s][:, j, :], func=ACT.Square, accum_out=pnorm_sq[:, j : j + 1]
-                )
-            inv = const.tile([P, PACK], F32, name="inv_pnorm%d" % s)
-            nc.gpsimd.tensor_tensor(out=inv[:], in0=pnorm_sq[:], in1=minus_half[:], op=ALU.pow)
-            inv_pnorm[s] = inv
-        regroup_prototypes(0)
-        regroup_prototypes(1)
-        quantise_prototypes(0)
-        quantise_prototypes(1)
+        def norm_on_scalar(s, j):
+            squares = unread.tile([P, C], BF16)
+            nc.scalar.activation(
+                out=squares[:], in_=prot_of[s][:, j, :], func=ACT.Square, accum_out=pnorm_sq[s][:, j : j + 1]
+            )
+
+        def norm_on_vector(s, j):
+            products = unread.tile([P, C], F32)
+            nc.vector.scalar_tensor_tensor(
+                out=products[:],
+                in0=prot_of[s][:, j, :],
+                scalar=1.0,
+                in1=prot_of[s][:, j, :],
+                op0=ALU.mult,
+                op1=ALU.mult,
+                accum_out=pnorm_sq[s][:, j : j + 1],
+            )
+
+        def invert_norms(s):
+            nc.gpsimd.tensor_tensor(out=inv_pnorm[s][:], in0=pnorm_sq[s][:], in1=minus_half[:], op=ALU.pow)
 
         scaled_of = {}
         grouped_of = {}
@@ -138,60 +166,65 @@ def tile_globalprototype_t_kernel(tc, features, prototypes, grad_out, out):
         scales_of = {}
 
         def scale_grad(chunk, s):
-            b, part = divmod(chunk, CHUNKS_PER_BATCH)
             if s == 0:
                 scaled = quant.tile([P, PASSES, PACK, CHUNK], BF16)
                 scaled_of[chunk] = scaled
             for j in range(PACK):
                 nc.vector.tensor_scalar(
                     out=scaled_of[chunk][:, s, j, :],
-                    in0=grad_of[b][:, s, j, part * CHUNK : (part + 1) * CHUNK],
+                    in0=grad_of[chunk][:, s, j, :],
                     scalar1=inv_pnorm[s][:, j : j + 1],
                     scalar2=None,
                     op0=ALU.mult,
                 )
-            if part == CHUNKS_PER_BATCH - 1 and s == PASSES - 1 and b + 2 < B:
-                load_grad(b + 2)
+            if s == PASSES - 1 and chunk + LOADS_AHEAD < CHUNKS:
+                load_grad(chunk + LOADS_AHEAD)
 
-        def regroup_grad(chunk, s):
-            if s == 0:
+        def regroup_grad(chunk, s, half, regroup):
+            if chunk not in grouped_of:
                 grouped = quant.tile([P, PASSES * CHUNK * PACK], BF16, align_bytes=64)
                 grouped_of[chunk] = grouped
             by_pass = grouped_of[chunk][:].rearrange("p (s w t) -> p s w t", s=PASSES, t=PACK)
-            regroup(by_pass[:, s], scaled_of[chunk][:, s])
+            cols = slice(half * HALF, (half + 1) * HALF)
+            regroup(by_pass[:, s, cols, :], scaled_of[chunk][:, s, :, cols])
 
-        def regroup_grad_on_gpsimd(chunk, s, half):
-            if s == 0 and half == 0:
-                grouped = quant.tile([P, PASSES * CHUNK * PACK], BF16, align_bytes=64)
-                grouped_of[chunk] = grouped
-            by_pass = grouped_of[chunk][:].rearrange("p (s w t) -> p s w t", s=PASSES, t=PACK)
-            cols = slice(half * (CHUNK // 2), (half + 1) * (CHUNK // 2))
-            nc.gpsimd.tensor_scalar(
-                out=by_pass[:, s, cols, :],
-                in0=scaled_of[chunk][:, s, :, cols].rearrange("p t w -> p w t"),
-                scalar1=1.0,
-                scalar2=0.0,
-                op0=ALU.mult,
-                op1=ALU.add,
+        def quantise_grad(chunk, first, width):
+            if chunk not in codes_of:
+                codes = quant.tile([P, PASSES * CHUNK], U32, align_bytes=64, bufs=3)
+                scales = quant.tile([P, PASSES * CHUNK], U8, align_bytes=64, bufs=3)
+                codes_of[chunk] = codes
+                scales_of[chunk] = scales
+            nc.vector.quantize_mx(
+                out=codes_of[chunk][:, first : first + width].bitcast(E5M2_X4),
+                scales=scales_of[chunk][:, first : first + width],
+                in_=grouped_of[chunk][:, first * PACK : (first + width) * PACK],
             )
 
-        def quantise_grad(chunk):
-            codes = quant.tile([P, PASSES * CHUNK], U32, align_bytes=64, bufs=CHUNKS_AHEAD + 1)
-            scales = quant.tile([P, PASSES * CHUNK], U8, align_bytes=64, bufs=CHUNKS_AHEAD + 1)
-            nc.vector.quantize_mx(out=codes[:].bitcast(E5M2_X4), scales=scales[:], in_=grouped_of[chunk][:])
-            codes_of[chunk] = codes
-            scales_of[chunk] = scales
-
+        for j in range(PACK):
+            norm_on_scalar(0, j)
+        regroup_prototypes(0, 1, regroup_on_gpsimd)
+        regroup_prototypes(0, 0, regroup_on_vector)
+        quantise_prototypes(0, 0)
+        invert_norms(0)
+        for j in range(PACK - 1):
+            norm_on_scalar(1, j)
+        regroup_prototypes(1, 0, regroup_on_vector)
+        norm_on_vector(1, PACK - 1)
+        regroup_prototypes(1, 1, regroup_on_gpsimd)
         scale_grad(0, 0)
-        regroup_grad(0, 0)
-        scale_grad(1, 0)
-        regroup_grad(1, 0)
+        regroup_grad(0, 0, 0, regroup_on_vector)
+        quantise_prototypes(1, 0)
+        quantise_prototypes(0, 1)
+        invert_norms(1)
+        regroup_grad(0, 0, 1, regroup_on_gpsimd)
         scale_grad(0, 1)
-        regroup_grad(0, 1)
-        scale_grad(1, 1)
-        quantise_grad(0)
-        regroup_grad(1, 1)
-        quantise_grad(1)
+        regroup_grad(0, 1, 0, regroup_on_vector)
+        quantise_prototypes(1, 1)
+        for s in range(PASSES):
+            quantise_grad(0, s * CHUNK, HALF)
+        regroup_grad(0, 1, 1, regroup_on_gpsimd)
+        for s in range(PASSES):
+            scale_grad(1, s)
 
         feat_t_of = {}
         inv_fnorm_of = {}
@@ -201,14 +234,16 @@ def tile_globalprototype_t_kernel(tc, features, prototypes, grad_out, out):
         out_sb_of = {}
 
         def transpose_features(blk):
-            b, q = divmod(blk, BLOCKS_PER_BATCH)
+            chunk, r = divmod(blk, BLOCKS_PER_CHUNK)
             feat_t = psum_ft.tile([P, C], BF16)
             for i in range(C_TILES):
                 nc.tensor.transpose(
                     out=feat_t[:, i * P : (i + 1) * P],
-                    in_=feat_of[b][:, i, q * P : (q + 1) * P],
+                    in_=feat_of[chunk][:, i, r * P : (r + 1) * P],
                     identity=ident_bf16[:],
                 )
+            if r == BLOCKS_PER_CHUNK - 1 and chunk + LOADS_AHEAD < CHUNKS:
+                load_features(chunk + LOADS_AHEAD)
             squares = unread.tile([P, C], BF16)
             fnorm_sq = stats.tile([P, 1], F32)
             nc.scalar.activation(out=squares[:], in_=feat_t[:], func=ACT.Square, accum_out=fnorm_sq[:])
@@ -223,7 +258,7 @@ def tile_globalprototype_t_kernel(tc, features, prototypes, grad_out, out):
         def multiply(blk):
             chunk, r = divmod(blk, BLOCKS_PER_CHUNK)
             ms = work.tile([P, C], F32)
-            for h in range(C // BANK):
+            for h in range(C_HALVES):
                 acc = psum_m.tile([P, BANK], F32)
                 for s in range(PASSES):
                     pixels = slice(s * CHUNK + r * P, s * CHUNK + (r + 1) * P)
@@ -290,7 +325,7 @@ def tile_globalprototype_t_kernel(tc, features, prototypes, grad_out, out):
             if r == 0:
                 out_sb = stores.tile([P, C_TILES, STORE], F32)
                 out_sb_of[store] = out_sb
-            for h in range(C_TILES // per_bank):
+            for h in range(C_HALVES):
                 flipped = psum_out.tile([P, BANK], F32)
                 flipped_of[(blk, h)] = flipped
                 for i in range(per_bank):
@@ -306,7 +341,7 @@ def tile_globalprototype_t_kernel(tc, features, prototypes, grad_out, out):
         def finish_result(blk):
             store, r = divmod(blk, BLOCKS_PER_STORE)
             b, part = divmod(store, N // STORE)
-            for h in range(C_TILES // per_bank):
+            for h in range(C_HALVES):
                 if vector_empties(blk, h):
                     empty_result_bank(blk, h)
             if r == BLOCKS_PER_STORE - 1:
@@ -316,32 +351,38 @@ def tile_globalprototype_t_kernel(tc, features, prototypes, grad_out, out):
 
         def gs_tasks(step, kind):
             found = []
-            for chunk in range(CHUNKS_AHEAD, CHUNKS):
-                u = step - BLOCKS_PER_CHUNK * (chunk - CHUNKS_AHEAD)
+            for chunk in range(FIRST_PLANNED_CHUNK, CHUNKS):
+                u = step - BLOCKS_PER_CHUNK * (chunk - FIRST_PLANNED_CHUNK)
                 for when, what, args in GS_PLAN:
                     if when == u and what == kind:
                         found.append((chunk,) + args)
             return found
 
         for step in range(BLOCKS + 4):
-            for chunk, s, half in gs_tasks(step, "regroup"):
-                regroup_grad_on_gpsimd(chunk, s, half)
             if 0 <= step - 4:
                 finish_result(step - 4)
             if step < BLOCKS:
                 transpose_features(step)
+            if step < PASSES:
+                regroup_grad(1, step, 1, regroup_on_gpsimd)
+            for chunk, s, half in gs_tasks(step, "regroup"):
+                regroup_grad(chunk, s, half, regroup_on_gpsimd)
             if 0 <= step - 1 < BLOCKS:
                 multiply(step - 1)
             if 0 <= step - 2 < BLOCKS:
                 projection_coefficient(step - 2)
+            if step == 0:
+                for s in range(PASSES):
+                    quantise_grad(0, s * CHUNK + HALF, HALF)
+            if step < PASSES:
+                regroup_grad(1, step, 0, regroup_on_vector)
             for chunk, s in gs_tasks(step, "scale"):
                 scale_grad(chunk, s)
+            if step == 1:
+                quantise_grad(1, 0, PASSES * CHUNK)
             for (chunk,) in gs_tasks(step, "quantise"):
-                quantise_grad(chunk)
+                quantise_grad(chunk, 0, PASSES * CHUNK)
             if 0 <= step - 2 < BLOCKS:
                 subtract_projection(step - 2)
             if 0 <= step - 3 < BLOCKS:
                 transpose_result(step - 3)
-            b, q = divmod(step, BLOCKS_PER_BATCH)
-            if b + 2 < B and q == BLOCKS_PER_BATCH - 1:
-                load_features(b + 2)

@@ -30,15 +30,16 @@ STORE = 256
 BLOCKS_PER_STORE = STORE // P
 
 GS_PLAN = (
-    (0, "scale", (0,)),
-    (1, "scale", (1,)),
-    (1, "regroup", (0, 0)),
-    (2, "regroup", (0, 1)),
-    (3, "regroup", (1, 0)),
-    (4, "regroup", (1, 1)),
-    (6, "quantise", ()),
+    (2, "scale", (0,)),
+    (3, "scale", (1,)),
+    (3, "regroup", (0, 0)),
+    (4, "regroup", (0, 1)),
+    (5, "regroup", (1, 0)),
+    (6, "regroup", (1, 1)),
+    (8, "quantise", ()),
 )
 FIRST_PLANNED_CHUNK = 2
+EARLY_BLOCKS = 4
 
 FLOPS = 2 * B * N * K * C
 
@@ -59,7 +60,7 @@ def tile_globalprototype_t_kernel(tc, features, prototypes, grad_out, out):
         unread = stack.enter_context(tc.tile_pool(name="unread", bufs=2))
         stats = stack.enter_context(tc.tile_pool(name="stats", bufs=6))
         stores = stack.enter_context(tc.tile_pool(name="stores", bufs=3))
-        psum_ft = stack.enter_context(tc.psum_pool(name="psum_ft", bufs=4))
+        psum_ft = stack.enter_context(tc.psum_pool(name="psum_ft", bufs=EARLY_BLOCKS))
         psum_m = stack.enter_context(tc.psum_pool(name="psum_m", bufs=2))
         psum_out = stack.enter_context(tc.psum_pool(name="psum_out", bufs=2))
         stack.enter_context(tc.manual_schedule())
@@ -200,31 +201,21 @@ def tile_globalprototype_t_kernel(tc, features, prototypes, grad_out, out):
                 in_=grouped_of[chunk][:, first * PACK : (first + width) * PACK],
             )
 
-        for j in range(PACK):
-            norm_on_scalar(0, j)
-        regroup_prototypes(0, 1, regroup_on_gpsimd)
-        regroup_prototypes(0, 0, regroup_on_vector)
-        quantise_prototypes(0, 0)
-        invert_norms(0)
-        for j in range(PACK - 1):
-            norm_on_scalar(1, j)
-        regroup_prototypes(1, 0, regroup_on_vector)
-        norm_on_vector(1, PACK - 1)
-        regroup_prototypes(1, 1, regroup_on_gpsimd)
-        scale_grad(0, 0)
-        regroup_grad(0, 0, 0, regroup_on_vector)
-        quantise_prototypes(1, 0)
-        quantise_prototypes(0, 1)
-        invert_norms(1)
-        regroup_grad(0, 0, 1, regroup_on_gpsimd)
-        scale_grad(0, 1)
-        regroup_grad(0, 1, 0, regroup_on_vector)
-        quantise_prototypes(1, 1)
+        for s in range(PASSES):
+            for j in range(PACK):
+                norm_on_scalar(s, j)
+            invert_norms(s)
+        for s in range(PASSES):
+            for h in range(C_HALVES):
+                regroup_prototypes(s, h, regroup_on_vector)
+        for s in range(PASSES):
+            for h in range(C_HALVES):
+                quantise_prototypes(s, h)
+        for s in range(PASSES):
+            scale_grad(0, s)
+            regroup_grad(0, s, 0, regroup_on_vector)
         for s in range(PASSES):
             quantise_grad(0, s * CHUNK, HALF)
-        regroup_grad(0, 1, 1, regroup_on_gpsimd)
-        for s in range(PASSES):
-            scale_grad(1, s)
 
         feat_t_of = {}
         inv_fnorm_of = {}
@@ -295,21 +286,26 @@ def tile_globalprototype_t_kernel(tc, features, prototypes, grad_out, out):
 
         def subtract_projection(blk):
             neg_res = work.tile([P, C], F32)
-            nc.vector.scalar_tensor_tensor(
-                out=neg_res[:],
-                in0=feat_t_of[blk][:],
-                scalar=coef_of[blk][:, 0:1],
-                in1=ms_of[blk][:],
-                op0=ALU.mult,
-                op1=ALU.subtract,
-            )
+            pieces = C_HALVES if blk == BLOCKS - 1 else 1
+            for cols in [slice(i * C // pieces, (i + 1) * C // pieces) for i in range(pieces)]:
+                nc.vector.scalar_tensor_tensor(
+                    out=neg_res[:, cols],
+                    in0=feat_t_of[blk][:, cols],
+                    scalar=coef_of[blk][:, 0:1],
+                    in1=ms_of[blk][:, cols],
+                    op0=ALU.mult,
+                    op1=ALU.subtract,
+                )
             neg_res_of[blk] = neg_res
 
         per_bank = BANK // P
         flipped_of = {}
 
         def vector_empties(blk, h):
-            return blk % 2 == 1 and h == 1
+            return blk % 2 == 1 and h == 1 and (blk < BLOCKS - 4 or blk == BLOCKS - 1)
+
+        def stored_by_banks(blk):
+            return blk >= BLOCKS - BLOCKS_PER_STORE
 
         def empty_result_bank(blk, h):
             store, r = divmod(blk, BLOCKS_PER_STORE)
@@ -319,6 +315,11 @@ def tile_globalprototype_t_kernel(tc, features, prototypes, grad_out, out):
                 nc.vector.tensor_scalar(out=dst, in0=src, scalar1=-1.0, scalar2=None, op0=ALU.mult)
             else:
                 nc.scalar.activation(out=dst, in_=src, func=ACT.Copy, scale=-1.0)
+            if stored_by_banks(blk):
+                b, first = divmod(blk * P, N)
+                nc.sync.dma_start(
+                    out=out_dram[b][:, h * per_bank : (h + 1) * per_bank, first : first + P], in_=dst
+                )
 
         def transpose_result(blk):
             store, r = divmod(blk, BLOCKS_PER_STORE)
@@ -344,7 +345,7 @@ def tile_globalprototype_t_kernel(tc, features, prototypes, grad_out, out):
             for h in range(C_HALVES):
                 if vector_empties(blk, h):
                     empty_result_bank(blk, h)
-            if r == BLOCKS_PER_STORE - 1:
+            if r == BLOCKS_PER_STORE - 1 and not stored_by_banks(blk):
                 nc.sync.dma_start(
                     out=out_dram[b][:, :, part * STORE : (part + 1) * STORE], in_=out_sb_of[store][:]
                 )
@@ -358,27 +359,34 @@ def tile_globalprototype_t_kernel(tc, features, prototypes, grad_out, out):
                         found.append((chunk,) + args)
             return found
 
+        for blk in range(EARLY_BLOCKS):
+            transpose_features(blk)
         for step in range(BLOCKS + 4):
-            if 0 <= step - 4:
-                finish_result(step - 4)
-            if step < BLOCKS:
-                transpose_features(step)
-            if step < PASSES:
-                regroup_grad(1, step, 1, regroup_on_gpsimd)
+            if step in (1, 2):
+                for half in range(2):
+                    regroup_grad(1, step - 1, half, regroup_on_gpsimd)
             for chunk, s, half in gs_tasks(step, "regroup"):
                 regroup_grad(chunk, s, half, regroup_on_gpsimd)
+            if 0 <= step - 4:
+                finish_result(step - 4)
+            if EARLY_BLOCKS <= step < BLOCKS:
+                transpose_features(step)
             if 0 <= step - 1 < BLOCKS:
                 multiply(step - 1)
             if 0 <= step - 2 < BLOCKS:
                 projection_coefficient(step - 2)
             if step == 0:
                 for s in range(PASSES):
+                    regroup_grad(0, s, 1, regroup_on_vector)
+                for s in range(PASSES):
                     quantise_grad(0, s * CHUNK + HALF, HALF)
-            if step < PASSES:
-                regroup_grad(1, step, 0, regroup_on_vector)
+                for chunk in (1, 2):
+                    for s in range(PASSES):
+                        scale_grad(chunk, s)
             for chunk, s in gs_tasks(step, "scale"):
-                scale_grad(chunk, s)
-            if step == 1:
+                if chunk > 2:
+                    scale_grad(chunk, s)
+            if step == BLOCKS_PER_CHUNK:
                 quantise_grad(1, 0, PASSES * CHUNK)
             for (chunk,) in gs_tasks(step, "quantise"):
                 quantise_grad(chunk, 0, PASSES * CHUNK)

@@ -30,15 +30,15 @@ STORE = 256
 BLOCKS_PER_STORE = STORE // P
 
 GS_PLAN = (
-    (2, "scale", (0,)),
-    (3, "scale", (1,)),
-    (3, "regroup", (0, 0)),
-    (4, "regroup", (0, 1)),
-    (5, "regroup", (1, 0)),
-    (6, "regroup", (1, 1)),
+    (4, "scale", (0,)),
+    (4, "regroup", (0, 0)),
+    (5, "regroup", (0, 1)),
+    (6, "scale", (1,)),
+    (6, "regroup", (1, 0)),
+    (7, "regroup", (1, 1)),
     (8, "quantise", ()),
 )
-FIRST_PLANNED_CHUNK = 2
+FIRST_PLANNED_CHUNK = 1
 EARLY_BLOCKS = 4
 
 FLOPS = 2 * B * N * K * C
@@ -353,20 +353,15 @@ def tile_globalprototype_t_kernel(tc, features, prototypes, grad_out, out):
         def gs_tasks(step, kind):
             found = []
             for chunk in range(FIRST_PLANNED_CHUNK, CHUNKS):
-                u = step - BLOCKS_PER_CHUNK * (chunk - FIRST_PLANNED_CHUNK)
+                start = BLOCKS_PER_CHUNK * (chunk - 2)
                 for when, what, args in GS_PLAN:
-                    if when == u and what == kind:
+                    if max(start + when, 0) == step and what == kind:
                         found.append((chunk,) + args)
             return found
 
         for blk in range(EARLY_BLOCKS):
             transpose_features(blk)
         for step in range(BLOCKS + 4):
-            if step in (1, 2):
-                for half in range(2):
-                    regroup_grad(1, step - 1, half, regroup_on_gpsimd)
-            for chunk, s, half in gs_tasks(step, "regroup"):
-                regroup_grad(chunk, s, half, regroup_on_gpsimd)
             if 0 <= step - 4:
                 finish_result(step - 4)
             if EARLY_BLOCKS <= step < BLOCKS:
@@ -380,16 +375,12 @@ def tile_globalprototype_t_kernel(tc, features, prototypes, grad_out, out):
                     regroup_grad(0, s, 1, regroup_on_vector)
                 for s in range(PASSES):
                     quantise_grad(0, s * CHUNK + HALF, HALF)
-                for chunk in (1, 2):
-                    for s in range(PASSES):
-                        scale_grad(chunk, s)
-            for chunk, s in gs_tasks(step, "scale"):
-                if chunk > 2:
-                    scale_grad(chunk, s)
-            if step == BLOCKS_PER_CHUNK:
-                quantise_grad(1, 0, PASSES * CHUNK)
             for (chunk,) in gs_tasks(step, "quantise"):
                 quantise_grad(chunk, 0, PASSES * CHUNK)
+            for chunk, s in gs_tasks(step, "scale"):
+                scale_grad(chunk, s)
+            for chunk, s, half in gs_tasks(step, "regroup"):
+                regroup_grad(chunk, s, half, regroup_on_gpsimd)
             if 0 <= step - 2 < BLOCKS:
                 subtract_projection(step - 2)
             if 0 <= step - 3 < BLOCKS:

@@ -71,6 +71,8 @@ def tile_globalprototype_t_kernel(tc, features, prototypes, grad_out, out):
         make_identity(nc, ident_f32[:])
         minus_half = const.tile([P, PACK], F32)
         nc.gpsimd.memset(minus_half[:], -0.5)
+        zeros = const.tile([P, BANK], F32)
+        nc.gpsimd.memset(zeros[:], 0.0)
 
         grad_of = {}
         feat_of = {}
@@ -302,7 +304,9 @@ def tile_globalprototype_t_kernel(tc, features, prototypes, grad_out, out):
         flipped_of = {}
 
         def vector_empties(blk, h):
-            return blk % 2 == 1 and h == 1 and (blk < BLOCKS - 4 or blk == BLOCKS - 1)
+            if blk == BLOCKS - 1:
+                return h == 1
+            return h == 0 and blk % 2 == 0 and 4 <= blk < BLOCKS - 3
 
         def stored_by_banks(blk):
             return blk >= BLOCKS - BLOCKS_PER_STORE
@@ -312,7 +316,14 @@ def tile_globalprototype_t_kernel(tc, features, prototypes, grad_out, out):
             dst = out_sb_of[store][:, h * per_bank : (h + 1) * per_bank, r * P : (r + 1) * P]
             src = flipped_of[(blk, h)][:].rearrange("p (i n) -> p i n", i=per_bank)
             if vector_empties(blk, h):
-                nc.vector.tensor_scalar(out=dst, in0=src, scalar1=-1.0, scalar2=None, op0=ALU.mult)
+                nc.vector.scalar_tensor_tensor(
+                    out=dst,
+                    in0=src,
+                    scalar=-1.0,
+                    in1=zeros[:].rearrange("p (i n) -> p i n", i=per_bank),
+                    op0=ALU.mult,
+                    op1=ALU.add,
+                )
             else:
                 nc.scalar.activation(out=dst, in_=src, func=ACT.Copy, scale=-1.0)
             if stored_by_banks(blk):
@@ -361,15 +372,17 @@ def tile_globalprototype_t_kernel(tc, features, prototypes, grad_out, out):
 
         for blk in range(EARLY_BLOCKS):
             transpose_features(blk)
-        for step in range(BLOCKS + 4):
-            if 0 <= step - 4:
-                finish_result(step - 4)
+        for step in range(BLOCKS + 3):
             if EARLY_BLOCKS <= step < BLOCKS:
                 transpose_features(step)
             if 0 <= step - 1 < BLOCKS:
                 multiply(step - 1)
+            if 0 <= step - 3 < BLOCKS:
+                transpose_result(step - 3)
             if 0 <= step - 2 < BLOCKS:
                 projection_coefficient(step - 2)
+            if 0 <= step - 3 < BLOCKS:
+                finish_result(step - 3)
             if step == 0:
                 for s in range(PASSES):
                     regroup_grad(0, s, 1, regroup_on_vector)
@@ -383,5 +396,3 @@ def tile_globalprototype_t_kernel(tc, features, prototypes, grad_out, out):
                 regroup_grad(chunk, s, half, regroup_on_gpsimd)
             if 0 <= step - 2 < BLOCKS:
                 subtract_projection(step - 2)
-            if 0 <= step - 3 < BLOCKS:
-                transpose_result(step - 3)

@@ -39,6 +39,7 @@ GS_PLAN = (
     (8, "quantise", ()),
 )
 FIRST_PLANNED_CHUNK = 1
+AS_MATMULS = 6
 EARLY_BLOCKS = 4
 
 FLOPS = 2 * B * N * K * C
@@ -230,11 +231,20 @@ def tile_globalprototype_t_kernel(tc, features, prototypes, grad_out, out):
             chunk, r = divmod(blk, BLOCKS_PER_CHUNK)
             feat_t = psum_ft.tile([P, C], BF16)
             for i in range(C_TILES):
-                nc.tensor.transpose(
-                    out=feat_t[:, i * P : (i + 1) * P],
-                    in_=feat_of[chunk][:, i, r * P : (r + 1) * P],
-                    identity=ident_bf16[:],
-                )
+                if i < C_TILES - AS_MATMULS:
+                    nc.tensor.transpose(
+                        out=feat_t[:, i * P : (i + 1) * P],
+                        in_=feat_of[chunk][:, i, r * P : (r + 1) * P],
+                        identity=ident_bf16[:],
+                    )
+                else:
+                    nc.tensor.matmul(
+                        out=feat_t[:, i * P : (i + 1) * P],
+                        lhsT=feat_of[chunk][:, i, r * P : (r + 1) * P],
+                        rhs=ident_bf16[:],
+                        start=True,
+                        stop=True,
+                    )
             if r == BLOCKS_PER_CHUNK - 1 and chunk + LOADS_AHEAD < CHUNKS:
                 load_features(chunk + LOADS_AHEAD)
             squares = unread.tile([P, C], BF16)

@@ -39,7 +39,9 @@ GS_PLAN = (
     (8, "quantise", ()),
 )
 FIRST_PLANNED_CHUNK = 1
-AS_MATMULS = 6
+AS_MATMULS = 2
+TENSOR_SUMS_EVERY = 2
+FAR_BELOW = -(2.0 ** 126)
 EARLY_BLOCKS = 4
 
 FLOPS = 2 * B * N * K * C
@@ -74,6 +76,10 @@ def tile_globalprototype_t_kernel(tc, features, prototypes, grad_out, out):
         nc.gpsimd.memset(minus_half[:], -0.5)
         zeros = const.tile([P, BANK], F32)
         nc.gpsimd.memset(zeros[:], 0.0)
+        off_diagonal = const.tile([P, P], BF16)
+        nc.gpsimd.tensor_scalar(
+            out=off_diagonal[:], in0=ident_bf16[:], scalar1=-FAR_BELOW, scalar2=FAR_BELOW, op0=ALU.mult, op1=ALU.add
+        )
 
         grad_of = {}
         feat_of = {}
@@ -227,9 +233,41 @@ def tile_globalprototype_t_kernel(tc, features, prototypes, grad_out, out):
         neg_res_of = {}
         out_sb_of = {}
 
+        bank_of = {}
+        fnorm_sq_of = {}
+
+        def summed_by_tensor(blk):
+            return blk >= EARLY_BLOCKS and blk % TENSOR_SUMS_EVERY == 0
+
+        def open_bank(blk):
+            bank = psum_ft.tile([P, BANK], F32)
+            bank_of[blk] = bank
+            feat_t_of[blk] = bank[:].bitcast(BF16)
+
+        def sum_squares_on_tensor(blk):
+            chunk, r = divmod(blk, BLOCKS_PER_CHUNK)
+            pixels = slice(r * P, (r + 1) * P)
+            open_bank(blk)
+            sums = bank_of[blk][:, 0:P]
+            nc.tensor.matmul(out=sums, lhsT=ident_bf16[:], rhs=off_diagonal[:], start=True, stop=False)
+            for i in range(C_TILES):
+                nc.tensor.matmul(
+                    out=sums,
+                    lhsT=feat_of[chunk][:, i, pixels],
+                    rhs=feat_of[chunk][:, i, pixels],
+                    start=False,
+                    stop=(i == C_TILES - 1),
+                )
+            diagonal = unread.tile([P, P], BF16)
+            fnorm_sq = stats.tile([P, 1], F32, name="fnorm_sq")
+            nc.scalar.activation(out=diagonal[:], in_=sums, func=ACT.Relu, accum_out=fnorm_sq[:])
+            fnorm_sq_of[blk] = fnorm_sq
+
         def transpose_features(blk):
             chunk, r = divmod(blk, BLOCKS_PER_CHUNK)
-            feat_t = psum_ft.tile([P, C], BF16)
+            if blk not in bank_of:
+                open_bank(blk)
+            feat_t = feat_t_of[blk]
             for i in range(C_TILES):
                 if i < C_TILES - AS_MATMULS:
                     nc.tensor.transpose(
@@ -247,14 +285,17 @@ def tile_globalprototype_t_kernel(tc, features, prototypes, grad_out, out):
                     )
             if r == BLOCKS_PER_CHUNK - 1 and chunk + LOADS_AHEAD < CHUNKS:
                 load_features(chunk + LOADS_AHEAD)
-            squares = unread.tile([P, C], BF16)
-            fnorm_sq = stats.tile([P, 1], F32)
-            nc.scalar.activation(out=squares[:], in_=feat_t[:], func=ACT.Square, accum_out=fnorm_sq[:])
+
+        def feature_norms(blk):
+            if not summed_by_tensor(blk):
+                squares = unread.tile([P, C], BF16)
+                fnorm_sq = stats.tile([P, 1], F32, name="fnorm_sq")
+                nc.scalar.activation(out=squares[:], in_=feat_t_of[blk], func=ACT.Square, accum_out=fnorm_sq[:])
+                fnorm_sq_of[blk] = fnorm_sq
             inv_fnorm = stats.tile([P, 1], F32)
-            nc.gpsimd.tensor_tensor(out=inv_fnorm[:], in0=fnorm_sq[:], in1=minus_half[:, 0:1], op=ALU.pow)
+            nc.gpsimd.tensor_tensor(out=inv_fnorm[:], in0=fnorm_sq_of[blk][:], in1=minus_half[:, 0:1], op=ALU.pow)
             inv_fsq = stats.tile([P, 1], F32)
             nc.gpsimd.tensor_tensor(out=inv_fsq[:], in0=inv_fnorm[:], in1=inv_fnorm[:], op=ALU.mult)
-            feat_t_of[blk] = feat_t
             inv_fnorm_of[blk] = inv_fnorm
             inv_fsq_of[blk] = inv_fsq
 
@@ -287,7 +328,7 @@ def tile_globalprototype_t_kernel(tc, features, prototypes, grad_out, out):
             coef = stats.tile([P, 1], F32)
             nc.vector.scalar_tensor_tensor(
                 out=products[:],
-                in0=feat_t_of[blk][:],
+                in0=feat_t_of[blk],
                 scalar=inv_fsq_of[blk][:, 0:1],
                 in1=ms_of[blk][:],
                 op0=ALU.mult,
@@ -316,7 +357,7 @@ def tile_globalprototype_t_kernel(tc, features, prototypes, grad_out, out):
         def vector_empties(blk, h):
             if blk == BLOCKS - 1:
                 return h == 1
-            return h == 0 and blk % 2 == 0 and 4 <= blk < BLOCKS - 3
+            return h == 0 and blk % 8 == 4 and 4 <= blk < BLOCKS - 3
 
         def stored_by_banks(blk):
             return blk >= BLOCKS - BLOCKS_PER_STORE
@@ -382,13 +423,20 @@ def tile_globalprototype_t_kernel(tc, features, prototypes, grad_out, out):
 
         for blk in range(EARLY_BLOCKS):
             transpose_features(blk)
+            feature_norms(blk)
         for step in range(BLOCKS + 3):
             if EARLY_BLOCKS <= step < BLOCKS:
-                transpose_features(step)
+                if not summed_by_tensor(step):
+                    transpose_features(step)
+                feature_norms(step)
             if 0 <= step - 1 < BLOCKS:
                 multiply(step - 1)
+            if step < BLOCKS and summed_by_tensor(step):
+                transpose_features(step)
             if 0 <= step - 3 < BLOCKS:
                 transpose_result(step - 3)
+            if step + 1 < BLOCKS and summed_by_tensor(step + 1):
+                sum_squares_on_tensor(step + 1)
             if 0 <= step - 2 < BLOCKS:
                 projection_coefficient(step - 2)
             if 0 <= step - 3 < BLOCKS:

@@ -357,7 +357,7 @@ def tile_globalprototype_t_kernel(tc, features, prototypes, grad_out, out):
         def vector_empties(blk, h):
             if blk == BLOCKS - 1:
                 return h == 1
-            return h == 0 and blk % 8 == 4 and 4 <= blk < BLOCKS - 3
+            return h == 0 and blk % 16 == 4 and 4 <= blk < BLOCKS - 3
 
         def stored_by_banks(blk):
             return blk >= BLOCKS - BLOCKS_PER_STORE

from contextlib import ExitStack

import concourse.mybir as mybir
from concourse.masks import make_identity

BF16 = mybir.dt.bfloat16
F32 = mybir.dt.float32
U32 = mybir.dt.uint32
U8 = mybir.dt.uint8
E4M3_X4 = mybir.dt.float8_e4m3fn_x4
E5M2_X4 = mybir.dt.float8_e5m2_x4
ALU = mybir.AluOpType
ACT = mybir.ActivationFunctionType

B, C, K, N = 4, 1024, 1024, 1024
P = 128
PACK = 4
PASSES = K // (P * PACK)
BANK = 512
C_TILES = C // P
C_HALVES = C // BANK
BLOCKS = B * N // P
CHUNK = 512
HALF = CHUNK // 2
BLOCKS_PER_CHUNK = CHUNK // P
CHUNKS_PER_BATCH = N // CHUNK
CHUNKS = B * CHUNKS_PER_BATCH
LOADS_AHEAD = 4
STORE = 256
BLOCKS_PER_STORE = STORE // P

GS_PLAN = (
    (4, "scale", (0,)),
    (4, "regroup", (0, 0)),
    (5, "regroup", (0, 1)),
    (6, "scale", (1,)),
    (6, "regroup", (1, 0)),
    (7, "regroup", (1, 1)),
    (8, "quantise", ()),
)
FIRST_PLANNED_CHUNK = 1
AS_MATMULS = 2
TENSOR_SUMS_EVERY = 2
FAR_BELOW = -(2.0 ** 126)
EARLY_BLOCKS = 4

FLOPS = 2 * B * N * K * C


def tile_globalprototype_t_kernel(tc, features, prototypes, grad_out, out):
    nc = tc.nc

    feat_dram = features.rearrange("b (i p) h w -> b p i (h w)", p=P)
    out_dram = out.rearrange("b (i p) h w -> b p i (h w)", p=P)
    grad_dram = grad_out.rearrange("b (s p j) h w -> b s p j (h w)", s=PASSES, p=P, j=PACK)
    prot_dram = prototypes.rearrange("(s p j) c -> s p j c", s=PASSES, p=P, j=PACK)

    with ExitStack() as stack:
        const = stack.enter_context(tc.tile_pool(name="const", bufs=1))
        loads = stack.enter_context(tc.tile_pool(name="loads", bufs=LOADS_AHEAD))
        quant = stack.enter_context(tc.tile_pool(name="quant", bufs=2))
        work = stack.enter_context(tc.tile_pool(name="work", bufs=3))
        unread = stack.enter_context(tc.tile_pool(name="unread", bufs=2))
        stats = stack.enter_context(tc.tile_pool(name="stats", bufs=6))
        stores = stack.enter_context(tc.tile_pool(name="stores", bufs=3))
        psum_ft = stack.enter_context(tc.psum_pool(name="psum_ft", bufs=EARLY_BLOCKS))
        psum_m = stack.enter_context(tc.psum_pool(name="psum_m", bufs=2))
        psum_out = stack.enter_context(tc.psum_pool(name="psum_out", bufs=2))
        stack.enter_context(tc.manual_schedule())

        ident_bf16 = const.tile([P, P], BF16)
        make_identity(nc, ident_bf16[:])
        ident_f32 = const.tile([P, P], F32)
        make_identity(nc, ident_f32[:])
        minus_half = const.tile([P, PACK], F32)
        nc.gpsimd.memset(minus_half[:], -0.5)
        zeros = const.tile([P, BANK], F32)
        nc.gpsimd.memset(zeros[:], 0.0)
        off_diagonal = const.tile([P, P], BF16)
        nc.gpsimd.tensor_scalar(
            out=off_diagonal[:], in0=ident_bf16[:], scalar1=-FAR_BELOW, scalar2=FAR_BELOW, op0=ALU.mult, op1=ALU.add
        )

        grad_of = {}
        feat_of = {}

        def pixels_of(chunk):
            b, part = divmod(chunk, CHUNKS_PER_BATCH)
            return b, slice(part * CHUNK, (part + 1) * CHUNK)

        def load_grad(chunk):
            b, cols = pixels_of(chunk)
            grad_sb = loads.tile([P, PASSES, PACK, CHUNK], BF16)
            for s in range(PASSES):
                nc.sync.dma_start(out=grad_sb[:, s], in_=grad_dram[b, s][:, :, cols])
            grad_of[chunk] = grad_sb

        def load_features(chunk):
            b, cols = pixels_of(chunk)
            feat_sb = loads.tile([P, C_TILES, CHUNK], BF16)
            nc.sync.dma_start(out=feat_sb[:], in_=feat_dram[b][:, :, cols])
            feat_of[chunk] = feat_sb

        prot_of = {}
        for s in range(PASSES):
            prot_sb = const.tile([P, PACK, C], BF16, name="prot_sb%d" % s)
            for rows in (slice(0, PACK // 2), slice(PACK // 2, PACK)):
                nc.sync.dma_start(out=prot_sb[:, rows], in_=prot_dram[s][:, rows])
            prot_of[s] = prot_sb
        for chunk in range(LOADS_AHEAD):
            load_grad(chunk)
            load_features(chunk)

        def regroup_on_vector(grouped, rows):
            nc.vector.tensor_copy(
                out=grouped.rearrange("p (c i) t -> p c t i", i=4),
                in_=rows.rearrange("p t (c i) -> p c t i", i=4),
            )

        def regroup_on_gpsimd(grouped, rows):
            nc.gpsimd.tensor_scalar(
                out=grouped,
                in0=rows.rearrange("p t w -> p w t"),
                scalar1=1.0,
                scalar2=0.0,
                op0=ALU.mult,
                op1=ALU.add,
            )

        prot_codes = const.tile([P, PASSES * C], U32, align_bytes=64)
        prot_scales = const.tile([P, PASSES * C], U8, align_bytes=64)
        prot_grouped = {}
        pnorm_sq = {}
        inv_pnorm = {}
        for s in range(PASSES):
            prot_grouped[s] = const.tile([P, C * PACK], BF16, align_bytes=64, name="prot_grouped%d" % s)
            pnorm_sq[s] = const.tile([P, PACK], F32, name="pnorm_sq%d" % s)
            inv_pnorm[s] = const.tile([P, PACK], F32, name="inv_pnorm%d" % s)

        def regroup_prototypes(s, h, regroup):
            by_word = prot_grouped[s][:].rearrange("p (w t) -> p w t", t=PACK)
            regroup(by_word[:, h * BANK : (h + 1) * BANK, :], prot_of[s][:, :, h * BANK : (h + 1) * BANK])

        def quantise_prototypes(s, h):
            cols = slice(s * C + h * BANK, s * C + (h + 1) * BANK)
            nc.vector.quantize_mx(
                out=prot_codes[:, cols].bitcast(E4M3_X4),
                scales=prot_scales[:, cols],
                in_=prot_grouped[s][:, h * BANK * PACK : (h + 1) * BANK * PACK],
            )

        def norm_on_scalar(s, j):
            squares = unread.tile([P, C], BF16)
            nc.scalar.activation(
                out=squares[:], in_=prot_of[s][:, j, :], func=ACT.Square, accum_out=pnorm_sq[s][:, j : j + 1]
            )

        def norm_on_vector(s, j):
            products = unread.tile([P, C], F32)
            nc.vector.scalar_tensor_tensor(
                out=products[:],
                in0=prot_of[s][:, j, :],
                scalar=1.0,
                in1=prot_of[s][:, j, :],
                op0=ALU.mult,
                op1=ALU.mult,
                accum_out=pnorm_sq[s][:, j : j + 1],
            )

        def invert_norms(s):
            nc.gpsimd.tensor_tensor(out=inv_pnorm[s][:], in0=pnorm_sq[s][:], in1=minus_half[:], op=ALU.pow)

        scaled_of = {}
        grouped_of = {}
        codes_of = {}
        scales_of = {}

        def scale_grad(chunk, s):
            if s == 0:
                scaled = quant.tile([P, PASSES, PACK, CHUNK], BF16)
                scaled_of[chunk] = scaled
            for j in range(PACK):
                nc.vector.tensor_scalar(
                    out=scaled_of[chunk][:, s, j, :],
                    in0=grad_of[chunk][:, s, j, :],
                    scalar1=inv_pnorm[s][:, j : j + 1],
                    scalar2=None,
                    op0=ALU.mult,
                )
            if s == PASSES - 1 and chunk + LOADS_AHEAD < CHUNKS:
                load_grad(chunk + LOADS_AHEAD)

        def regroup_grad(chunk, s, half, regroup):
            if chunk not in grouped_of:
                grouped = quant.tile([P, PASSES * CHUNK * PACK], BF16, align_bytes=64)
                grouped_of[chunk] = grouped
            by_pass = grouped_of[chunk][:].rearrange("p (s w t) -> p s w t", s=PASSES, t=PACK)
            cols = slice(half * HALF, (half + 1) * HALF)
            regroup(by_pass[:, s, cols, :], scaled_of[chunk][:, s, :, cols])

        def quantise_grad(chunk, first, width):
            if chunk not in codes_of:
                codes = quant.tile([P, PASSES * CHUNK], U32, align_bytes=64, bufs=3)
                scales = quant.tile([P, PASSES * CHUNK], U8, align_bytes=64, bufs=3)
                codes_of[chunk] = codes
                scales_of[chunk] = scales
            nc.vector.quantize_mx(
                out=codes_of[chunk][:, first : first + width].bitcast(E5M2_X4),
                scales=scales_of[chunk][:, first : first + width],
                in_=grouped_of[chunk][:, first * PACK : (first + width) * PACK],
            )

        for s in range(PASSES):
            for j in range(PACK):
                norm_on_scalar(s, j)
            invert_norms(s)
        for s in range(PASSES):
            for h in range(C_HALVES):
                regroup_prototypes(s, h, regroup_on_vector)
        for s in range(PASSES):
            for h in range(C_HALVES):
                quantise_prototypes(s, h)
        for s in range(PASSES):
            scale_grad(0, s)
            regroup_grad(0, s, 0, regroup_on_vector)
        for s in range(PASSES):
            quantise_grad(0, s * CHUNK, HALF)

        feat_t_of = {}
        inv_fnorm_of = {}
        inv_fsq_of = {}
        ms_of = {}
        neg_res_of = {}
        out_sb_of = {}

        bank_of = {}
        fnorm_sq_of = {}

        def summed_by_tensor(blk):
            return blk >= EARLY_BLOCKS and blk % TENSOR_SUMS_EVERY == 0

        def open_bank(blk):
            bank = psum_ft.tile([P, BANK], F32)
            bank_of[blk] = bank
            feat_t_of[blk] = bank[:].bitcast(BF16)

        def sum_squares_on_tensor(blk):
            chunk, r = divmod(blk, BLOCKS_PER_CHUNK)
            pixels = slice(r * P, (r + 1) * P)
            open_bank(blk)
            sums = bank_of[blk][:, 0:P]
            nc.tensor.matmul(out=sums, lhsT=ident_bf16[:], rhs=off_diagonal[:], start=True, stop=False)
            for i in range(C_TILES):
                nc.tensor.matmul(
                    out=sums,
                    lhsT=feat_of[chunk][:, i, pixels],
                    rhs=feat_of[chunk][:, i, pixels],
                    start=False,
                    stop=(i == C_TILES - 1),
                )
            diagonal = unread.tile([P, P], BF16)
            fnorm_sq = stats.tile([P, 1], F32, name="fnorm_sq")
            nc.scalar.activation(out=diagonal[:], in_=sums, func=ACT.Relu, accum_out=fnorm_sq[:])
            fnorm_sq_of[blk] = fnorm_sq

        def transpose_features(blk):
            chunk, r = divmod(blk, BLOCKS_PER_CHUNK)
            if blk not in bank_of:
                open_bank(blk)
            feat_t = feat_t_of[blk]
            for i in range(C_TILES):
                if i < C_TILES - AS_MATMULS:
                    nc.tensor.transpose(
                        out=feat_t[:, i * P : (i + 1) * P],
                        in_=feat_of[chunk][:, i, r * P : (r + 1) * P],
                        identity=ident_bf16[:],
                    )
                else:
                    nc.tensor.matmul(
                        out=feat_t[:, i * P : (i + 1) * P],
                        lhsT=feat_of[chunk][:, i, r * P : (r + 1) * P],
                        rhs=ident_bf16[:],
                        start=True,
                        stop=True,
                    )
            if r == BLOCKS_PER_CHUNK - 1 and chunk + LOADS_AHEAD < CHUNKS:
                load_features(chunk + LOADS_AHEAD)

        def feature_norms(blk):
            if not summed_by_tensor(blk):
                squares = unread.tile([P, C], BF16)
                fnorm_sq = stats.tile([P, 1], F32, name="fnorm_sq")
                nc.scalar.activation(out=squares[:], in_=feat_t_of[blk], func=ACT.Square, accum_out=fnorm_sq[:])
                fnorm_sq_of[blk] = fnorm_sq
            inv_fnorm = stats.tile([P, 1], F32)
            nc.gpsimd.tensor_tensor(out=inv_fnorm[:], in0=fnorm_sq_of[blk][:], in1=minus_half[:, 0:1], op=ALU.pow)
            inv_fsq = stats.tile([P, 1], F32)
            nc.gpsimd.tensor_tensor(out=inv_fsq[:], in0=inv_fnorm[:], in1=inv_fnorm[:], op=ALU.mult)
            inv_fnorm_of[blk] = inv_fnorm
            inv_fsq_of[blk] = inv_fsq

        def multiply(blk):
            chunk, r = divmod(blk, BLOCKS_PER_CHUNK)
            ms = work.tile([P, C], F32)
            for h in range(C_HALVES):
                acc = psum_m.tile([P, BANK], F32)
                for s in range(PASSES):
                    pixels = slice(s * CHUNK + r * P, s * CHUNK + (r + 1) * P)
                    channels = slice(s * C + h * BANK, s * C + (h + 1) * BANK)
                    nc.tensor.matmul_mx(
                        out=acc[:],
                        lhsT=codes_of[chunk][:, pixels].bitcast(E5M2_X4),
                        lhsT_scale=scales_of[chunk][:, pixels],
                        rhs=prot_codes[:, channels].bitcast(E4M3_X4),
                        rhs_scale=prot_scales[:, channels],
                        start=(s == 0),
                        stop=(s == PASSES - 1),
                    )
                nc.scalar.activation(
                    out=ms[:, h * BANK : (h + 1) * BANK], in_=acc[:], func=ACT.Copy, scale=inv_fnorm_of[blk][:, 0:1]
                )
            ms_of[blk] = ms

        coef_of = {}

        def projection_coefficient(blk):
            products = unread.tile([P, C], F32)
            coef = stats.tile([P, 1], F32)
            nc.vector.scalar_tensor_tensor(
                out=products[:],
                in0=feat_t_of[blk],
                scalar=inv_fsq_of[blk][:, 0:1],
                in1=ms_of[blk][:],
                op0=ALU.mult,
                op1=ALU.mult,
                accum_out=coef[:],
            )
            coef_of[blk] = coef

        def subtract_projection(blk):
            neg_res = work.tile([P, C], F32)
            pieces = C_HALVES if blk == BLOCKS - 1 else 1
            for cols in [slice(i * C // pieces, (i + 1) * C // pieces) for i in range(pieces)]:
                nc.vector.scalar_tensor_tensor(
                    out=neg_res[:, cols],
                    in0=feat_t_of[blk][:, cols],
                    scalar=coef_of[blk][:, 0:1],
                    in1=ms_of[blk][:, cols],
                    op0=ALU.mult,
                    op1=ALU.subtract,
                )
            neg_res_of[blk] = neg_res

        per_bank = BANK // P
        flipped_of = {}

        def vector_empties(blk, h):
            if blk == BLOCKS - 1:
                return h == 1
            return h == 0 and blk % 16 == 4 and 4 <= blk < BLOCKS - 3

        def stored_by_banks(blk):
            return blk >= BLOCKS - BLOCKS_PER_STORE

        def empty_result_bank(blk, h):
            store, r = divmod(blk, BLOCKS_PER_STORE)
            dst = out_sb_of[store][:, h * per_bank : (h + 1) * per_bank, r * P : (r + 1) * P]
            src = flipped_of[(blk, h)][:].rearrange("p (i n) -> p i n", i=per_bank)
            if vector_empties(blk, h):
                nc.vector.scalar_tensor_tensor(
                    out=dst,
                    in0=src,
                    scalar=-1.0,
                    in1=zeros[:].rearrange("p (i n) -> p i n", i=per_bank),
                    op0=ALU.mult,
                    op1=ALU.add,
                )
            else:
                nc.scalar.activation(out=dst, in_=src, func=ACT.Copy, scale=-1.0)
            if stored_by_banks(blk):
                b, first = divmod(blk * P, N)
                nc.sync.dma_start(
                    out=out_dram[b][:, h * per_bank : (h + 1) * per_bank, first : first + P], in_=dst
                )

        def transpose_result(blk):
            store, r = divmod(blk, BLOCKS_PER_STORE)
            if r == 0:
                out_sb = stores.tile([P, C_TILES, STORE], F32)
                out_sb_of[store] = out_sb
            for h in range(C_HALVES):
                flipped = psum_out.tile([P, BANK], F32)
                flipped_of[(blk, h)] = flipped
                for i in range(per_bank):
                    c_tile = h * per_bank + i
                    nc.tensor.transpose(
                        out=flipped[:, i * P : (i + 1) * P],
                        in_=neg_res_of[blk][:, c_tile * P : (c_tile + 1) * P],
                        identity=ident_f32[:],
                    )
                if not vector_empties(blk, h):
                    empty_result_bank(blk, h)

        def finish_result(blk):
            store, r = divmod(blk, BLOCKS_PER_STORE)
            b, part = divmod(store, N // STORE)
            for h in range(C_HALVES):
                if vector_empties(blk, h):
                    empty_result_bank(blk, h)
            if r == BLOCKS_PER_STORE - 1 and not stored_by_banks(blk):
                nc.sync.dma_start(
                    out=out_dram[b][:, :, part * STORE : (part + 1) * STORE], in_=out_sb_of[store][:]
                )

        def gs_tasks(step, kind):
            found = []
            for chunk in range(FIRST_PLANNED_CHUNK, CHUNKS):
                start = BLOCKS_PER_CHUNK * (chunk - 2)
                for when, what, args in GS_PLAN:
                    if max(start + when, 0) == step and what == kind:
                        found.append((chunk,) + args)
            return found

        for blk in range(EARLY_BLOCKS):
            transpose_features(blk)
            feature_norms(blk)
        for step in range(BLOCKS + 3):
            if EARLY_BLOCKS <= step < BLOCKS:
                if not summed_by_tensor(step):
                    transpose_features(step)
                feature_norms(step)
            if 0 <= step - 1 < BLOCKS:
                multiply(step - 1)
            if step < BLOCKS and summed_by_tensor(step):
                transpose_features(step)
            if 0 <= step - 3 < BLOCKS:
                transpose_result(step - 3)
            if step + 1 < BLOCKS and summed_by_tensor(step + 1):
                sum_squares_on_tensor(step + 1)
            if 0 <= step - 2 < BLOCKS:
                projection_coefficient(step - 2)
            if 0 <= step - 3 < BLOCKS:
                finish_result(step - 3)
            if step == 0:
                for s in range(PASSES):
                    regroup_grad(0, s, 1, regroup_on_vector)
                for s in range(PASSES):
                    quantise_grad(0, s * CHUNK + HALF, HALF)
            for (chunk,) in gs_tasks(step, "quantise"):
                quantise_grad(chunk, 0, PASSES * CHUNK)
            for chunk, s in gs_tasks(step, "scale"):
                scale_grad(chunk, s)
            for chunk, s, half in gs_tasks(step, "regroup"):
                regroup_grad(chunk, s, half, regroup_on_gpsimd)
            if 0 <= step - 2 < BLOCKS:
                subtract_projection(step - 2)
